import numpy as np
import ml_dtypes


def mxq(x, axis, fmt="e4m3"):
    dtype, down = {"e4m3": (ml_dtypes.float8_e4m3fn, 7), "e5m2": (ml_dtypes.float8_e5m2, 14)}[fmt]
    v = np.moveaxis(np.asarray(x, np.float32).astype(ml_dtypes.bfloat16).astype(np.float64), axis, -1)
    blocks = v.reshape(v.shape[:-1] + (-1, 32))
    amax = np.abs(blocks).max(-1, keepdims=True)
    byte = np.maximum(np.where(amax > 0, np.frexp(amax)[1] - 1 + 127, 0) - down, 1)
    scale = np.exp2(byte - 127.0)
    codes = (blocks / scale).astype(np.float32).astype(dtype).astype(np.float64)
    return np.moveaxis((codes * scale).reshape(v.shape), -1, axis)


WIDE = False


def mx_kscale(k):
    if not WIDE:
        return np.ones(k)
    levels = np.array([10, -10, 5, -5, 0])
    a = np.random.permutation(np.resize(levels, k // 512 * 4)).reshape(k // 512, 4)
    idx = np.arange(k)
    return np.exp2(a[idx // 512, idx % 128 // 32])


BF16 = ml_dtypes.bfloat16


def bf(x):
    return np.asarray(x, np.float32).astype(BF16)


def f64(x):
    return np.asarray(x).astype(np.float64)


B, I, O = 2048, 512, 512
GRID_SIZE = 5
SPLINE_ORDER = 3
NUM_BASIS = GRID_SIZE + SPLINE_ORDER
K = I * NUM_BASIS
GRID = np.linspace(-1.0, 1.0, GRID_SIZE + 2 * SPLINE_ORDER + 1)
EPS = 1e-6
X0 = 0.5 * np.log(2.0 / (GRID[1] - GRID[0]))


def bspline_basis(x):
    xe = x[..., None]
    bas = ((xe >= GRID[:-1]) & (xe < GRID[1:])).astype(np.float64)
    for k in range(1, SPLINE_ORDER + 1):
        nb = bas.shape[-1] - 1
        g_i = GRID[:nb]
        g_i1 = GRID[1:1 + nb]
        g_ik = GRID[k:k + nb]
        g_ik1 = GRID[k + 1:k + 1 + nb]
        dl = g_ik - g_i
        dr = g_ik1 - g_i1
        left = np.where(dl > EPS, (xe - g_i) / np.where(dl > EPS, dl, 1.0), 0.0) * bas[..., :nb]
        right = np.where(dr > EPS, (g_ik1 - xe) / np.where(dr > EPS, dr, 1.0), 0.0) * bas[..., 1:nb + 1]
        bas = left + right
    return bas[..., :NUM_BASIS]


def setup_inputs():
    a = np.log2(mx_kscale(K))[::NUM_BASIS]
    n = np.random.standard_normal((B, I))
    tail = -np.sign(a) * (X0 + np.abs(a) * np.log(2.0) / 3.0) + 0.15 * n
    c = np.exp2(2.0 * np.abs(a))
    return {"x": bf(np.where(a == 0, n, tail)),
            "spline_coeffs": bf(np.random.standard_normal((O, I, NUM_BASIS)) * (2.0 / np.sqrt(I)) * c[None, :, None])}


def reference(x, spline_coeffs):
    xn = np.tanh(f64(x))
    basis = bspline_basis(xn)
    bq = mxq(basis.reshape(B, K), 1, "e4m3")
    wq = mxq(f64(spline_coeffs).reshape(O, K), 1, "e4m3")
    return bq @ wq.T

@@ -1,0 +1,209 @@
+import math
+from contextlib import ExitStack
+
+import concourse.mybir as mybir
+from concourse.masks import make_identity
+
+FLOPS = 2 * 2048 * 4096 * 512
+
+F32 = mybir.dt.float32
+BF16 = mybir.dt.bfloat16
+I32 = mybir.dt.int32
+U32 = mybir.dt.uint32
+U8 = mybir.dt.uint8
+FP8X4 = mybir.dt.float8_e4m3fn_x4
+ALU = mybir.AluOpType
+ACTF = mybir.ActivationFunctionType
+
+P = 128
+SLOT = ((0, 7, 2, 5), (4, 3, 6, 1))
+R6 = 1.0 / math.sqrt(6.0)
+R23 = math.sqrt(2.0 / 3.0)
+
+
+def tile_kan_layer_kernel(tc, x, spline_coeffs, out):
+    nc = tc.nc
+    with ExitStack() as ctx:
+        ctx.enter_context(nc.allow_non_contiguous_dma(reason="64-byte runs regroup the coefficients by feature class"))
+        const = ctx.enter_context(tc.tile_pool(name="const", bufs=1))
+        xpp = ctx.enter_context(tc.tile_pool(name="xpp", bufs=2))
+        wgp = ctx.enter_context(tc.tile_pool(name="wgp", bufs=2))
+        work = ctx.enter_context(tc.tile_pool(name="work", bufs=2))
+        idxp = ctx.enter_context(tc.tile_pool(name="idxp", bufs=3))
+        gtp = ctx.enter_context(tc.tile_pool(name="gtp", bufs=1))
+        cod = ctx.enter_context(tc.tile_pool(name="cod", bufs=2))
+        outp = ctx.enter_context(tc.tile_pool(name="outp", bufs=2))
+        psa = ctx.enter_context(tc.psum_pool(name="psa", bufs=1))
+        psx = ctx.enter_context(tc.psum_pool(name="psx", bufs=2))
+        psw = ctx.enter_context(tc.psum_pool(name="psw", bufs=2))
+
+        ident = const.tile([P, P], BF16, name="ident")
+        make_identity(nc, ident[:])
+
+        x_sb = const.tile([P, 16, 512], BF16, name="x_sb")
+        xv = x.rearrange("(p t) i -> p t i", t=16)
+        ov = out.rearrange("(p t) o -> p t o", t=16)
+        w_sb = [const.tile([P, 4, 1024], BF16, name="w_sb%d" % ot) for ot in range(4)]
+        wv = spline_coeffs.rearrange("(ot o) (g f s) k -> ot o f g (s k)", o=P, g=32, f=4, s=4)
+        w_codes = const.tile([P, 4, 2, 512], U32, name="w_codes", align_bytes=64)
+        w_scales = const.tile([P, 4, 2, 512], U8, name="w_scales", align_bytes=64)
+
+        ctx.enter_context(tc.manual_schedule())
+
+        def load_x(c):
+            nc.sync.dma_start(out=x_sb[:, 4 * c:4 * c + 4, :], in_=xv[:, 4 * c:4 * c + 4, :])
+
+        def load_w(f):
+            for ot in range(4):
+                nc.sync.dma_start(
+                    out=w_sb[ot][:, f, :].rearrange("o (g e) -> o g e", e=32),
+                    in_=wv[ot, :, f, :, :],
+                )
+
+        load_x(0)
+        load_w(0)
+        load_w(1)
+        load_x(1)
+        load_w(2)
+        load_w(3)
+        load_x(2)
+        load_x(3)
+
+        st = {}
+
+        def xperm(c):
+            xp = xpp.tile([P, 4, 512], BF16, name="xp")
+            for j in range(4):
+                nc.scalar.copy(
+                    out=xp[:, j, :].rearrange("p (f g s) -> p f g s", f=4, g=32, s=4),
+                    in_=x_sb[:, 4 * c + j, :].rearrange("p (g f s) -> p f g s", g=32, f=4, s=4),
+                )
+            st[("xp", c)] = xp
+
+        def s0(u):
+            c, f = divmod(u, 4)
+            xp = st[("xp", c)]
+            px = psx.tile([P, 512], BF16, name="px")
+            for j in range(4):
+                nc.tensor.transpose(px[:, j * P:(j + 1) * P], xp[:, j, f * P:(f + 1) * P], ident[:])
+            sg = work.tile([P, 2, 512], F32, name="sg")
+            nc.scalar.activation(out=sg[:, 0, :], in_=px[:], func=ACTF.Sigmoid, scale=2.0)
+            nc.scalar.activation(out=sg[:, 1, :], in_=px[:], func=ACTF.Sigmoid, scale=-2.0)
+            idx = idxp.tile([P, 2, 2, 512], U32, name="idx")
+            nc.scalar.activation(out=idx[:, 1], in_=sg[:], func=ACTF.Copy, scale=2.75)
+            nc.scalar.activation(out=idx[:, 0], in_=sg[:], func=ACTF.Copy, scale=2.75, bias=0.5)
+            st[("sg", u)] = sg
+            st[("idx", u)] = idx
+
+        def s1(u):
+            sg = st[("sg", u)]
+            idx = st[("idx", u)]
+            pp = work.tile([P, 2, 512], F32, name="pp")
+            nc.vector.scalar_tensor_tensor(out=pp[:], in0=sg[:], scalar=2.75, in1=idx[:, 1].bitcast(I32), op0=ALU.mult, op1=ALU.subtract)
+            nc.scalar.activation(out=pp[:], in_=pp[:], func=ACTF.Abs, scale=4.0)
+            sa = work.tile([P, 2, 512], F32, name="sa")
+            sb = work.tile([P, 2, 512], F32, name="sb")
+            sc = work.tile([P, 2, 512], F32, name="sc")
+            nc.scalar.activation(out=sa[:], in_=pp[:], func=ACTF.Square, scale=R6)
+            nc.scalar.activation(out=sc[:], in_=pp[:], func=ACTF.Square, scale=R23, bias=-R23)
+            nc.scalar.activation(out=sb[:], in_=pp[:], func=ACTF.Square, scale=-R6, bias=2.0 * R6)
+            st[("pp", u)] = (pp, sa, sb, sc)
+
+        def s3(u):
+            pp, sa, sb, sc = st[("pp", u)]
+            idx = st[("idx", u)]
+            nc.vector.tensor_tensor(out=sa[:], in0=pp[:], in1=sa[:], op=ALU.mult)
+            nc.vector.scalar_tensor_tensor(out=sc[:], in0=pp[:], scalar=-1.0, in1=sc[:], op0=ALU.add, op1=ALU.mult)
+            nc.vector.scalar_tensor_tensor(out=sb[:], in0=pp[:], scalar=-2.0, in1=sb[:], op0=ALU.add, op1=ALU.mult)
+            cv = work.tile([P, 2, 2, 512], BF16, name="cv")
+            nc.vector.scalar_tensor_tensor(out=cv[:, 0], in0=sc[:], scalar=0.0, in1=sa[:], op0=ALU.max, op1=ALU.subtract, reverse1=True)
+            nc.vector.scalar_tensor_tensor(out=cv[:, 1], in0=sc[:], scalar=0.0, in1=sb[:], op0=ALU.min, op1=ALU.subtract)
+            codes = cod.tile([P, 2, 512], U32, name="codes", align_bytes=64)
+            scl = cod.tile([P, 2, 512], U8, name="scl", align_bytes=64)
+            gts = []
+            for ps in range(2):
+                gt = gtp.tile([P, 512, 4], BF16, name="gt%d" % ps, align_bytes=64)
+                nc.vector.scalar_tensor_tensor(
+                    out=gt[:],
+                    in0=idx[:].bitcast(I32).rearrange("p v s b -> p b (v s)"),
+                    scalar=float(ps + 1),
+                    in1=cv[:].rearrange("p v s b -> p b (v s)"),
+                    op0=ALU.is_equal,
+                    op1=ALU.mult,
+                )
+                gts.append(gt)
+            for ps in range(2):
+                nc.vector.quantize_mx(
+                    out=codes[:, ps, :].bitcast(FP8X4),
+                    scales=scl[:, ps, :],
+                    in_=gts[ps][:].rearrange("p b t -> p (b t)"),
+                )
+            st[("codes", u)] = (codes, scl)
+
+        def prep_w_move(f):
+            wgs = []
+            for ps in range(2):
+                wg = wgp.tile([P, 512, 4], BF16, name="wg", align_bytes=64)
+                for ot in range(4):
+                    pw = psw.tile([P, 4, P], BF16, name="pw")
+                    wk = w_sb[ot][:, f, :].rearrange("o (j k) -> o j k", k=8)
+                    for t in range(4):
+                        nc.tensor.transpose(pw[:, t, :], wk[:, :, SLOT[ps][t]], ident[:])
+                    nc.scalar.copy(out=wg[:, ot * P:(ot + 1) * P, :], in_=pw[:].rearrange("p t o -> p o t"))
+                wgs.append(wg)
+            st[("wg", f)] = wgs
+
+        def prep_w_quant(f):
+            for ps in range(2):
+                nc.vector.quantize_mx(
+                    out=w_codes[:, f, ps, :].bitcast(FP8X4),
+                    scales=w_scales[:, f, ps, :],
+                    in_=st[("wg", f)][ps][:].rearrange("p o t -> p (o t)"),
+                )
+
+        def mm(u):
+            c, f = divmod(u, 4)
+            if f == 0:
+                st[("acc", c)] = [psa.tile([P, 512], F32, name="acc%d" % j) for j in range(4)]
+            acc = st[("acc", c)]
+            codes, scl = st[("codes", u)]
+            for ps in range(2):
+                for j in range(4):
+                    nc.tensor.matmul_mx(
+                        out=acc[j][:],
+                        lhsT=codes[:, ps, j * P:(j + 1) * P].bitcast(FP8X4),
+                        lhsT_scale=scl[:, ps, j * P:(j + 1) * P],
+                        rhs=w_codes[:, f, ps, :].bitcast(FP8X4),
+                        rhs_scale=w_scales[:, f, ps, :],
+                        start=(f == 0 and ps == 0),
+                        stop=(f == 3 and ps == 1),
+                    )
+
+        def evac(c):
+            acc = st[("acc", c)]
+            osb = outp.tile([P, 4, 512], F32, name="osb")
+            for j in range(4):
+                nc.scalar.copy(out=osb[:, j, :], in_=acc[j][:])
+            nc.sync.dma_start(out=ov[:, 4 * c:4 * c + 4, :], in_=osb[:])
+
+        NU = 16
+        xperm(0)
+        s0(0)
+        s0(1)
+        s1(0)
+        for i in range(NU):
+            if i + 2 < NU:
+                if (i + 2) % 4 == 0:
+                    xperm((i + 2) // 4)
+                s0(i + 2)
+            if i + 1 < NU:
+                s1(i + 1)
+            if i > 0 and i % 4 == 0:
+                evac(i // 4 - 1)
+            if i < 4:
+                prep_w_move(i)
+            s3(i)
+            if i < 4:
+                prep_w_quant(i)
+            mm(i)
+        evac(3)

@@ -31,7 +31,7 @@ def tile_kan_layer_kernel(tc, x, spline_coeffs, out):
         work = ctx.enter_context(tc.tile_pool(name="work", bufs=2))
         idxp = ctx.enter_context(tc.tile_pool(name="idxp", bufs=3))
         gtp = ctx.enter_context(tc.tile_pool(name="gtp", bufs=1))
-        cod = ctx.enter_context(tc.tile_pool(name="cod", bufs=2))
+        cod = ctx.enter_context(tc.tile_pool(name="cod", bufs=4))
         outp = ctx.enter_context(tc.tile_pool(name="outp", bufs=2))
         psa = ctx.enter_context(tc.psum_pool(name="psa", bufs=1))
         psx = ctx.enter_context(tc.psum_pool(name="psx", bufs=2))
@@ -74,7 +74,7 @@ def tile_kan_layer_kernel(tc, x, spline_coeffs, out):
         def xperm(c):
             xp = xpp.tile([P, 4, 512], BF16, name="xp")
             for j in range(4):
-                nc.scalar.copy(
+                (nc.vector.tensor_copy if c == 0 else nc.scalar.copy)(
                     out=xp[:, j, :].rearrange("p (f g s) -> p f g s", f=4, g=32, s=4),
                     in_=x_sb[:, 4 * c + j, :].rearrange("p (g f s) -> p f g s", g=32, f=4, s=4),
                 )
@@ -187,23 +187,27 @@ def tile_kan_layer_kernel(tc, x, spline_coeffs, out):
             nc.sync.dma_start(out=ov[:, 4 * c:4 * c + 4, :], in_=osb[:])
 
         NU = 16
+        LAG = 2
         xperm(0)
         s0(0)
         s0(1)
         s1(0)
-        for i in range(NU):
+        for i in range(NU + LAG):
             if i + 2 < NU:
                 if (i + 2) % 4 == 0:
                     xperm((i + 2) // 4)
                 s0(i + 2)
             if i + 1 < NU:
                 s1(i + 1)
-            if i > 0 and i % 4 == 0:
-                evac(i // 4 - 1)
-            if i < 4:
-                prep_w_move(i)
-            s3(i)
-            if i < 4:
-                prep_w_quant(i)
-            mm(i)
+            m = i - LAG
+            if m > 0 and m % 4 == 0:
+                evac(m // 4 - 1)
+            if 0 <= m < 4:
+                prep_w_move(m)
+            if i < NU:
+                s3(i)
+            if 0 <= m < 4:
+                prep_w_quant(m)
+            if m >= 0:
+                mm(m)
         evac(3)

@@ -91,7 +91,6 @@ def tile_kan_layer_kernel(tc, x, spline_coeffs, out):
             nc.scalar.activation(out=sg[:, 1, :], in_=px[:], func=ACTF.Sigmoid, scale=-2.0)
             idx = idxp.tile([P, 2, 2, 512], U32, name="idx")
             nc.scalar.activation(out=idx[:, 1], in_=sg[:], func=ACTF.Copy, scale=2.75)
-            nc.scalar.activation(out=idx[:, 0], in_=sg[:], func=ACTF.Copy, scale=2.75, bias=0.5)
             st[("sg", u)] = sg
             st[("idx", u)] = idx
 
@@ -107,17 +106,22 @@ def tile_kan_layer_kernel(tc, x, spline_coeffs, out):
             nc.scalar.activation(out=sa[:], in_=pp[:], func=ACTF.Square, scale=R6)
             nc.scalar.activation(out=sc[:], in_=pp[:], func=ACTF.Square, scale=R23, bias=-R23)
             nc.scalar.activation(out=sb[:], in_=pp[:], func=ACTF.Square, scale=-R6, bias=2.0 * R6)
+            nc.scalar.activation(out=idx[:, 0], in_=sg[:], func=ACTF.Copy, scale=2.75, bias=0.5)
             st[("pp", u)] = (pp, sa, sb, sc)
 
-        def s3(u):
+        def s3a(u):
             pp, sa, sb, sc = st[("pp", u)]
-            idx = st[("idx", u)]
-            nc.vector.tensor_tensor(out=sa[:], in0=pp[:], in1=sa[:], op=ALU.mult)
             nc.vector.scalar_tensor_tensor(out=sc[:], in0=pp[:], scalar=-1.0, in1=sc[:], op0=ALU.add, op1=ALU.mult)
+            nc.vector.tensor_tensor(out=sa[:], in0=pp[:], in1=sa[:], op=ALU.mult)
             nc.vector.scalar_tensor_tensor(out=sb[:], in0=pp[:], scalar=-2.0, in1=sb[:], op0=ALU.add, op1=ALU.mult)
             cv = work.tile([P, 2, 2, 512], BF16, name="cv")
             nc.vector.scalar_tensor_tensor(out=cv[:, 0], in0=sc[:], scalar=0.0, in1=sa[:], op0=ALU.max, op1=ALU.subtract, reverse1=True)
             nc.vector.scalar_tensor_tensor(out=cv[:, 1], in0=sc[:], scalar=0.0, in1=sb[:], op0=ALU.min, op1=ALU.subtract)
+            st[("cv", u)] = cv
+
+        def s3b(u):
+            idx = st[("idx", u)]
+            cv = st[("cv", u)]
             codes = cod.tile([P, 2, 512], U32, name="codes", align_bytes=64)
             scl = cod.tile([P, 2, 512], U8, name="scl", align_bytes=64)
             gts = []
@@ -182,30 +186,38 @@ def tile_kan_layer_kernel(tc, x, spline_coeffs, out):
         def evac(c):
             acc = st[("acc", c)]
             osb = outp.tile([P, 4, 512], F32, name="osb")
-            for j in range(4):
-                nc.scalar.copy(out=osb[:, j, :], in_=acc[j][:])
-            nc.sync.dma_start(out=ov[:, 4 * c:4 * c + 4, :], in_=osb[:])
+            if c < 3:
+                for j in range(4):
+                    nc.scalar.copy(out=osb[:, j, :], in_=acc[j][:])
+                nc.sync.dma_start(out=ov[:, 4 * c:4 * c + 4, :], in_=osb[:])
+            else:
+                for h in range(2):
+                    nc.scalar.copy(out=osb[:, 2 * h, :], in_=acc[2 * h][:])
+                    nc.vector.tensor_copy(out=osb[:, 2 * h + 1, :], in_=acc[2 * h + 1][:])
+                    nc.sync.dma_start(out=ov[:, 4 * c + 2 * h:4 * c + 2 * h + 2, :], in_=osb[:, 2 * h:2 * h + 2, :])
 
         NU = 16
         LAG = 2
         xperm(0)
         s0(0)
-        s0(1)
         s1(0)
+        s0(1)
         for i in range(NU + LAG):
             if i + 2 < NU:
                 if (i + 2) % 4 == 0:
                     xperm((i + 2) // 4)
                 s0(i + 2)
-            if i + 1 < NU:
-                s1(i + 1)
             m = i - LAG
             if m > 0 and m % 4 == 0:
                 evac(m // 4 - 1)
             if 0 <= m < 4:
                 prep_w_move(m)
             if i < NU:
-                s3(i)
+                s3a(i)
+            if i + 1 < NU:
+                s1(i + 1)
+            if i < NU:
+                s3b(i)
             if 0 <= m < 4:
                 prep_w_quant(m)
             if m >= 0:

@@ -94,55 +94,85 @@ def tile_kan_layer_kernel(tc, x, spline_coeffs, out):
             st[("sg", u)] = sg
             st[("idx", u)] = idx
 
-        def s1(u):
+        def resid(u):
             sg = st[("sg", u)]
             idx = st[("idx", u)]
             pp = work.tile([P, 2, 512], F32, name="pp")
             nc.vector.scalar_tensor_tensor(out=pp[:], in0=sg[:], scalar=2.75, in1=idx[:, 1].bitcast(I32), op0=ALU.mult, op1=ALU.subtract)
+            st[("pp", u)] = pp
+
+        def sq_first(u):
+            pp = st[("pp", u)]
             nc.scalar.activation(out=pp[:], in_=pp[:], func=ACTF.Abs, scale=4.0)
+            sc = work.tile([P, 2, 512], F32, name="sc")
+            nc.scalar.activation(out=sc[:], in_=pp[:], func=ACTF.Square, scale=R23, bias=-R23)
+            st[("sc", u)] = sc
+
+        def sq_rest(u):
+            pp = st[("pp", u)]
             sa = work.tile([P, 2, 512], F32, name="sa")
             sb = work.tile([P, 2, 512], F32, name="sb")
-            sc = work.tile([P, 2, 512], F32, name="sc")
             nc.scalar.activation(out=sa[:], in_=pp[:], func=ACTF.Square, scale=R6)
-            nc.scalar.activation(out=sc[:], in_=pp[:], func=ACTF.Square, scale=R23, bias=-R23)
             nc.scalar.activation(out=sb[:], in_=pp[:], func=ACTF.Square, scale=-R6, bias=2.0 * R6)
-            nc.scalar.activation(out=idx[:, 0], in_=sg[:], func=ACTF.Copy, scale=2.75, bias=0.5)
-            st[("pp", u)] = (pp, sa, sb, sc)
+            nc.scalar.activation(out=st[("idx", u)][:, 0], in_=st[("sg", u)][:], func=ACTF.Copy, scale=2.75, bias=0.5)
+            st[("sab", u)] = (sa, sb)
 
-        def s3a(u):
-            pp, sa, sb, sc = st[("pp", u)]
+        def quant(u, ps):
+            if ps == 0:
+                codes = cod.tile([P, 2, 512], U32, name="codes", align_bytes=64)
+                scl = cod.tile([P, 2, 512], U8, name="scl", align_bytes=64)
+                st[("codes", u)] = (codes, scl)
+            codes, scl = st[("codes", u)]
+            nc.vector.quantize_mx(
+                out=codes[:, ps, :].bitcast(FP8X4),
+                scales=scl[:, ps, :],
+                in_=st[("gt", u, ps)][:].rearrange("p b t -> p (b t)"),
+            )
+
+        def poly(u):
+            pp = st[("pp", u)]
+            sc = st[("sc", u)]
+            sa, sb = st[("sab", u)]
             nc.vector.scalar_tensor_tensor(out=sc[:], in0=pp[:], scalar=-1.0, in1=sc[:], op0=ALU.add, op1=ALU.mult)
+            if u > 0:
+                quant(u - 1, 0)
             nc.vector.tensor_tensor(out=sa[:], in0=pp[:], in1=sa[:], op=ALU.mult)
+            if u > 0:
+                quant(u - 1, 1)
             nc.vector.scalar_tensor_tensor(out=sb[:], in0=pp[:], scalar=-2.0, in1=sb[:], op0=ALU.add, op1=ALU.mult)
             cv = work.tile([P, 2, 2, 512], BF16, name="cv")
             nc.vector.scalar_tensor_tensor(out=cv[:, 0], in0=sc[:], scalar=0.0, in1=sa[:], op0=ALU.max, op1=ALU.subtract, reverse1=True)
             nc.vector.scalar_tensor_tensor(out=cv[:, 1], in0=sc[:], scalar=0.0, in1=sb[:], op0=ALU.min, op1=ALU.subtract)
             st[("cv", u)] = cv
 
-        def s3b(u):
-            idx = st[("idx", u)]
-            cv = st[("cv", u)]
-            codes = cod.tile([P, 2, 512], U32, name="codes", align_bytes=64)
-            scl = cod.tile([P, 2, 512], U8, name="scl", align_bytes=64)
-            gts = []
-            for ps in range(2):
-                gt = gtp.tile([P, 512, 4], BF16, name="gt%d" % ps, align_bytes=64)
-                nc.vector.scalar_tensor_tensor(
-                    out=gt[:],
-                    in0=idx[:].bitcast(I32).rearrange("p v s b -> p b (v s)"),
-                    scalar=float(ps + 1),
-                    in1=cv[:].rearrange("p v s b -> p b (v s)"),
-                    op0=ALU.is_equal,
-                    op1=ALU.mult,
-                )
-                gts.append(gt)
-            for ps in range(2):
-                nc.vector.quantize_mx(
-                    out=codes[:, ps, :].bitcast(FP8X4),
-                    scales=scl[:, ps, :],
-                    in_=gts[ps][:].rearrange("p b t -> p (b t)"),
-                )
-            st[("codes", u)] = (codes, scl)
+        def gate_planes(u):
+            gpl = gtp.tile([P, 4, 512], BF16, name="gpl")
+            nc.vector.scalar_tensor_tensor(
+                out=gpl[:].rearrange("p t b -> p (t b)"),
+                in0=st[("idx", u)][:].bitcast(I32).rearrange("p v s b -> p (v s b)"),
+                scalar=1.0,
+                in1=st[("cv", u)][:].rearrange("p v s b -> p (v s b)"),
+                op0=ALU.is_equal,
+                op1=ALU.mult,
+            )
+            st[("gpl", u)] = gpl
+
+        def weave(u):
+            gt = gtp.tile([P, 512, 4], BF16, name="gt0", align_bytes=64)
+            nc.scalar.copy(out=gt[:], in_=st[("gpl", u)][:].rearrange("p t b -> p b t"))
+            st[("gt", u, 0)] = gt
+
+        def gate_woven(u, ps):
+            gt = gtp.tile([P, 512, 4], BF16, name="gt%d" % ps, align_bytes=64)
+            nc.vector.scalar_tensor_tensor(
+                out=gt[:],
+                in0=st[("idx", u)][:].bitcast(I32).rearrange("p v s b -> p b (v s)"),
+                scalar=float(ps + 1),
+                in1=st[("cv", u)][:].rearrange("p v s b -> p b (v s)"),
+                op0=ALU.is_equal,
+                op1=ALU.mult,
+            )
+            st[("gt", u, ps)] = gt
 
         def prep_w_move(f):
             wgs = []
@@ -200,7 +230,9 @@ def tile_kan_layer_kernel(tc, x, spline_coeffs, out):
         LAG = 2
         xperm(0)
         s0(0)
-        s1(0)
+        resid(0)
+        sq_first(0)
+        sq_rest(0)
         s0(1)
         for i in range(NU + LAG):
             if i + 2 < NU:
@@ -213,11 +245,22 @@ def tile_kan_layer_kernel(tc, x, spline_coeffs, out):
             if 0 <= m < 4:
                 prep_w_move(m)
             if i < NU:
-                s3a(i)
+                poly(i)
+            if i == NU:
+                quant(NU - 1, 0)
+                quant(NU - 1, 1)
             if i + 1 < NU:
-                s1(i + 1)
+                resid(i + 1)
+                sq_first(i + 1)
+            if i < NU - 1:
+                gate_planes(i)
+                weave(i)
+            if i == NU - 1:
+                gate_woven(i, 0)
+            if i + 1 < NU:
+                sq_rest(i + 1)
             if i < NU:
-                s3b(i)
+                gate_woven(i, 1)
             if 0 <= m < 4:
                 prep_w_quant(m)
             if m >= 0:

@@ -48,7 +48,6 @@ def tile_kan_layer_kernel(tc, x, spline_coeffs, out):
         w_codes = const.tile([P, 4, 2, 512], U32, name="w_codes", align_bytes=64)
         w_scales = const.tile([P, 4, 2, 512], U8, name="w_scales", align_bytes=64)
 
-        ctx.enter_context(tc.manual_schedule())
 
         def load_x(c):
             nc.sync.dma_start(out=x_sb[:, 4 * c:4 * c + 4, :], in_=xv[:, 4 * c:4 * c + 4, :])
@@ -94,85 +93,55 @@ def tile_kan_layer_kernel(tc, x, spline_coeffs, out):
             st[("sg", u)] = sg
             st[("idx", u)] = idx
 
-        def resid(u):
+        def s1(u):
             sg = st[("sg", u)]
             idx = st[("idx", u)]
             pp = work.tile([P, 2, 512], F32, name="pp")
             nc.vector.scalar_tensor_tensor(out=pp[:], in0=sg[:], scalar=2.75, in1=idx[:, 1].bitcast(I32), op0=ALU.mult, op1=ALU.subtract)
-            st[("pp", u)] = pp
-
-        def sq_first(u):
-            pp = st[("pp", u)]
             nc.scalar.activation(out=pp[:], in_=pp[:], func=ACTF.Abs, scale=4.0)
-            sc = work.tile([P, 2, 512], F32, name="sc")
-            nc.scalar.activation(out=sc[:], in_=pp[:], func=ACTF.Square, scale=R23, bias=-R23)
-            st[("sc", u)] = sc
-
-        def sq_rest(u):
-            pp = st[("pp", u)]
             sa = work.tile([P, 2, 512], F32, name="sa")
             sb = work.tile([P, 2, 512], F32, name="sb")
+            sc = work.tile([P, 2, 512], F32, name="sc")
             nc.scalar.activation(out=sa[:], in_=pp[:], func=ACTF.Square, scale=R6)
+            nc.scalar.activation(out=sc[:], in_=pp[:], func=ACTF.Square, scale=R23, bias=-R23)
             nc.scalar.activation(out=sb[:], in_=pp[:], func=ACTF.Square, scale=-R6, bias=2.0 * R6)
-            nc.scalar.activation(out=st[("idx", u)][:, 0], in_=st[("sg", u)][:], func=ACTF.Copy, scale=2.75, bias=0.5)
-            st[("sab", u)] = (sa, sb)
+            nc.scalar.activation(out=idx[:, 0], in_=sg[:], func=ACTF.Copy, scale=2.75, bias=0.5)
+            st[("pp", u)] = (pp, sa, sb, sc)
 
-        def quant(u, ps):
-            if ps == 0:
-                codes = cod.tile([P, 2, 512], U32, name="codes", align_bytes=64)
-                scl = cod.tile([P, 2, 512], U8, name="scl", align_bytes=64)
-                st[("codes", u)] = (codes, scl)
-            codes, scl = st[("codes", u)]
-            nc.vector.quantize_mx(
-                out=codes[:, ps, :].bitcast(FP8X4),
-                scales=scl[:, ps, :],
-                in_=st[("gt", u, ps)][:].rearrange("p b t -> p (b t)"),
-            )
-
-        def poly(u):
-            pp = st[("pp", u)]
-            sc = st[("sc", u)]
-            sa, sb = st[("sab", u)]
+        def s3a(u):
+            pp, sa, sb, sc = st[("pp", u)]
             nc.vector.scalar_tensor_tensor(out=sc[:], in0=pp[:], scalar=-1.0, in1=sc[:], op0=ALU.add, op1=ALU.mult)
-            if u > 0:
-                quant(u - 1, 0)
             nc.vector.tensor_tensor(out=sa[:], in0=pp[:], in1=sa[:], op=ALU.mult)
-            if u > 0:
-                quant(u - 1, 1)
             nc.vector.scalar_tensor_tensor(out=sb[:], in0=pp[:], scalar=-2.0, in1=sb[:], op0=ALU.add, op1=ALU.mult)
             cv = work.tile([P, 2, 2, 512], BF16, name="cv")
             nc.vector.scalar_tensor_tensor(out=cv[:, 0], in0=sc[:], scalar=0.0, in1=sa[:], op0=ALU.max, op1=ALU.subtract, reverse1=True)
             nc.vector.scalar_tensor_tensor(out=cv[:, 1], in0=sc[:], scalar=0.0, in1=sb[:], op0=ALU.min, op1=ALU.subtract)
             st[("cv", u)] = cv
 
-        def gate_planes(u):
-            gpl = gtp.tile([P, 4, 512], BF16, name="gpl")
-            nc.vector.scalar_tensor_tensor(
-                out=gpl[:].rearrange("p t b -> p (t b)"),
-                in0=st[("idx", u)][:].bitcast(I32).rearrange("p v s b -> p (v s b)"),
-                scalar=1.0,
-                in1=st[("cv", u)][:].rearrange("p v s b -> p (v s b)"),
-                op0=ALU.is_equal,
-                op1=ALU.mult,
-            )
-            st[("gpl", u)] = gpl
-
-        def weave(u):
-            gt = gtp.tile([P, 512, 4], BF16, name="gt0", align_bytes=64)
-            nc.scalar.copy(out=gt[:], in_=st[("gpl", u)][:].rearrange("p t b -> p b t"))
-            st[("gt", u, 0)] = gt
-
-        def gate_woven(u, ps):
-            gt = gtp.tile([P, 512, 4], BF16, name="gt%d" % ps, align_bytes=64)
-            nc.vector.scalar_tensor_tensor(
-                out=gt[:],
-                in0=st[("idx", u)][:].bitcast(I32).rearrange("p v s b -> p b (v s)"),
-                scalar=float(ps + 1),
-                in1=st[("cv", u)][:].rearrange("p v s b -> p b (v s)"),
-                op0=ALU.is_equal,
-                op1=ALU.mult,
-            )
-            st[("gt", u, ps)] = gt
+        def s3b(u):
+            idx = st[("idx", u)]
+            cv = st[("cv", u)]
+            codes = cod.tile([P, 2, 512], U32, name="codes", align_bytes=64)
+            scl = cod.tile([P, 2, 512], U8, name="scl", align_bytes=64)
+            gts = []
+            for ps in range(2):
+                gt = gtp.tile([P, 512, 4], BF16, name="gt%d" % ps, align_bytes=64)
+                nc.vector.scalar_tensor_tensor(
+                    out=gt[:],
+                    in0=idx[:].bitcast(I32).rearrange("p v s b -> p b (v s)"),
+                    scalar=float(ps + 1),
+                    in1=cv[:].rearrange("p v s b -> p b (v s)"),
+                    op0=ALU.is_equal,
+                    op1=ALU.mult,
+                )
+                gts.append(gt)
+            for ps in range(2):
+                nc.vector.quantize_mx(
+                    out=codes[:, ps, :].bitcast(FP8X4),
+                    scales=scl[:, ps, :],
+                    in_=gts[ps][:].rearrange("p b t -> p (b t)"),
+                )
+            st[("codes", u)] = (codes, scl)
 
         def prep_w_move(f):
             wgs = []
@@ -230,9 +199,7 @@ def tile_kan_layer_kernel(tc, x, spline_coeffs, out):
         LAG = 2
         xperm(0)
         s0(0)
-        resid(0)
-        sq_first(0)
-        sq_rest(0)
+        s1(0)
         s0(1)
         for i in range(NU + LAG):
             if i + 2 < NU:
@@ -245,22 +212,11 @@ def tile_kan_layer_kernel(tc, x, spline_coeffs, out):
             if 0 <= m < 4:
                 prep_w_move(m)
             if i < NU:
-                poly(i)
-            if i == NU:
-                quant(NU - 1, 0)
-                quant(NU - 1, 1)
+                s3a(i)
             if i + 1 < NU:
-                resid(i + 1)
-                sq_first(i + 1)
-            if i < NU - 1:
-                gate_planes(i)
-                weave(i)
-            if i == NU - 1:
-                gate_woven(i, 0)
-            if i + 1 < NU:
-                sq_rest(i + 1)
+                s1(i + 1)
             if i < NU:
-                gate_woven(i, 1)
+                s3b(i)
             if 0 <= m < 4:
                 prep_w_quant(m)
             if m >= 0:

@@ -93,55 +93,85 @@ def tile_kan_layer_kernel(tc, x, spline_coeffs, out):
             st[("sg", u)] = sg
             st[("idx", u)] = idx
 
-        def s1(u):
+        def resid(u):
             sg = st[("sg", u)]
             idx = st[("idx", u)]
-            pp = work.tile([P, 2, 512], F32, name="pp")
+            pp = work.tile([P, 2, 512], F32, name="pp", bufs=3)
             nc.vector.scalar_tensor_tensor(out=pp[:], in0=sg[:], scalar=2.75, in1=idx[:, 1].bitcast(I32), op0=ALU.mult, op1=ALU.subtract)
+            st[("pp", u)] = pp
+
+        def sq_first(u):
+            pp = st[("pp", u)]
             nc.scalar.activation(out=pp[:], in_=pp[:], func=ACTF.Abs, scale=4.0)
+            sc = work.tile([P, 2, 512], F32, name="sc")
+            nc.scalar.activation(out=sc[:], in_=pp[:], func=ACTF.Square, scale=R23, bias=-R23)
+            st[("sc", u)] = sc
+
+        def sq_rest(u):
+            pp = st[("pp", u)]
             sa = work.tile([P, 2, 512], F32, name="sa")
             sb = work.tile([P, 2, 512], F32, name="sb")
-            sc = work.tile([P, 2, 512], F32, name="sc")
             nc.scalar.activation(out=sa[:], in_=pp[:], func=ACTF.Square, scale=R6)
-            nc.scalar.activation(out=sc[:], in_=pp[:], func=ACTF.Square, scale=R23, bias=-R23)
             nc.scalar.activation(out=sb[:], in_=pp[:], func=ACTF.Square, scale=-R6, bias=2.0 * R6)
-            nc.scalar.activation(out=idx[:, 0], in_=sg[:], func=ACTF.Copy, scale=2.75, bias=0.5)
-            st[("pp", u)] = (pp, sa, sb, sc)
+            nc.scalar.activation(out=st[("idx", u)][:, 0], in_=st[("sg", u)][:], func=ACTF.Copy, scale=2.75, bias=0.5)
+            st[("sab", u)] = (sa, sb)
 
-        def s3a(u):
-            pp, sa, sb, sc = st[("pp", u)]
+        def quant(u, ps):
+            if ("codes", u) not in st:
+                codes = cod.tile([P, 2, 512], U32, name="codes", align_bytes=64)
+                scl = cod.tile([P, 2, 512], U8, name="scl", align_bytes=64)
+                st[("codes", u)] = (codes, scl)
+            codes, scl = st[("codes", u)]
+            nc.vector.quantize_mx(
+                out=codes[:, ps, :].bitcast(FP8X4),
+                scales=scl[:, ps, :],
+                in_=st[("gt", u, ps)][:].rearrange("p b t -> p (b t)"),
+            )
+
+        def products(u):
+            pp = st[("pp", u)]
+            sc = st[("sc", u)]
+            sa, sb = st[("sab", u)]
             nc.vector.scalar_tensor_tensor(out=sc[:], in0=pp[:], scalar=-1.0, in1=sc[:], op0=ALU.add, op1=ALU.mult)
             nc.vector.tensor_tensor(out=sa[:], in0=pp[:], in1=sa[:], op=ALU.mult)
             nc.vector.scalar_tensor_tensor(out=sb[:], in0=pp[:], scalar=-2.0, in1=sb[:], op0=ALU.add, op1=ALU.mult)
+
+        def combine(u):
+            sc = st[("sc", u)]
+            sa, sb = st[("sab", u)]
             cv = work.tile([P, 2, 2, 512], BF16, name="cv")
             nc.vector.scalar_tensor_tensor(out=cv[:, 0], in0=sc[:], scalar=0.0, in1=sa[:], op0=ALU.max, op1=ALU.subtract, reverse1=True)
             nc.vector.scalar_tensor_tensor(out=cv[:, 1], in0=sc[:], scalar=0.0, in1=sb[:], op0=ALU.min, op1=ALU.subtract)
             st[("cv", u)] = cv
 
-        def s3b(u):
-            idx = st[("idx", u)]
-            cv = st[("cv", u)]
-            codes = cod.tile([P, 2, 512], U32, name="codes", align_bytes=64)
-            scl = cod.tile([P, 2, 512], U8, name="scl", align_bytes=64)
-            gts = []
-            for ps in range(2):
-                gt = gtp.tile([P, 512, 4], BF16, name="gt%d" % ps, align_bytes=64)
-                nc.vector.scalar_tensor_tensor(
-                    out=gt[:],
-                    in0=idx[:].bitcast(I32).rearrange("p v s b -> p b (v s)"),
-                    scalar=float(ps + 1),
-                    in1=cv[:].rearrange("p v s b -> p b (v s)"),
-                    op0=ALU.is_equal,
-                    op1=ALU.mult,
-                )
-                gts.append(gt)
-            for ps in range(2):
-                nc.vector.quantize_mx(
-                    out=codes[:, ps, :].bitcast(FP8X4),
-                    scales=scl[:, ps, :],
-                    in_=gts[ps][:].rearrange("p b t -> p (b t)"),
-                )
-            st[("codes", u)] = (codes, scl)
+        def gate_planes(u):
+            gpl = gtp.tile([P, 4, 512], BF16, name="gpl")
+            nc.vector.scalar_tensor_tensor(
+                out=gpl[:].rearrange("p t b -> p (t b)"),
+                in0=st[("idx", u)][:].bitcast(I32).rearrange("p v s b -> p (v s b)"),
+                scalar=1.0,
+                in1=st[("cv", u)][:].rearrange("p v s b -> p (v s b)"),
+                op0=ALU.is_equal,
+                op1=ALU.mult,
+            )
+            st[("gpl", u)] = gpl
+
+        def weave(u):
+            gt = gtp.tile([P, 512, 4], BF16, name="gt0", align_bytes=64)
+            nc.scalar.copy(out=gt[:], in_=st[("gpl", u)][:].rearrange("p t b -> p b t"))
+            st[("gt", u, 0)] = gt
+
+        def gate_woven(u, ps):
+            gt = gtp.tile([P, 512, 4], BF16, name="gt%d" % ps, align_bytes=64)
+            nc.vector.scalar_tensor_tensor(
+                out=gt[:],
+                in0=st[("idx", u)][:].bitcast(I32).rearrange("p v s b -> p b (v s)"),
+                scalar=float(ps + 1),
+                in1=st[("cv", u)][:].rearrange("p v s b -> p b (v s)"),
+                op0=ALU.is_equal,
+                op1=ALU.mult,
+            )
+            st[("gt", u, ps)] = gt
 
         def prep_w_move(f):
             wgs = []
@@ -199,24 +229,43 @@ def tile_kan_layer_kernel(tc, x, spline_coeffs, out):
         LAG = 2
         xperm(0)
         s0(0)
-        s1(0)
+        resid(0)
+        sq_first(0)
+        sq_rest(0)
         s0(1)
+        resid(1)
         for i in range(NU + LAG):
+            if 1 <= i < NU:
+                weave(i - 1)
             if i + 2 < NU:
                 if (i + 2) % 4 == 0:
                     xperm((i + 2) // 4)
                 s0(i + 2)
+            if i + 1 < NU:
+                sq_first(i + 1)
+                sq_rest(i + 1)
             m = i - LAG
             if m > 0 and m % 4 == 0:
                 evac(m // 4 - 1)
             if 0 <= m < 4:
                 prep_w_move(m)
             if i < NU:
-                s3a(i)
-            if i + 1 < NU:
-                s1(i + 1)
+                products(i)
+            if 1 <= i <= NU:
+                quant(i - 1, 1)
             if i < NU:
-                s3b(i)
+                combine(i)
+            if i + 2 < NU:
+                resid(i + 2)
+            if i < NU - 1:
+                gate_planes(i)
+            if i == NU - 1:
+                quant(i - 1, 0)
+                gate_woven(i, 0)
+            if i < NU:
+                gate_woven(i, 1)
+            if 1 <= i <= NU and i != NU - 1:
+                quant(i - 1, 0)
             if 0 <= m < 4:
                 prep_w_quant(m)
             if m >= 0:

@@ -8,7 +8,6 @@ FLOPS = 2 * 2048 * 4096 * 512
 
 F32 = mybir.dt.float32
 BF16 = mybir.dt.bfloat16
-I32 = mybir.dt.int32
 U32 = mybir.dt.uint32
 U8 = mybir.dt.uint8
 FP8X4 = mybir.dt.float8_e4m3fn_x4
@@ -16,9 +15,14 @@ ALU = mybir.AluOpType
 ACTF = mybir.ActivationFunctionType
 
 P = 128
-SLOT = ((0, 7, 2, 5), (4, 3, 6, 1))
-R6 = 1.0 / math.sqrt(6.0)
-R23 = math.sqrt(2.0 / 3.0)
+NU = 16
+LAG = 3
+WSTEP = 1
+SLOT = ((0, 7, 6, 1), (4, 3, 2, 5))
+
+
+def knot_x(k):
+    return 0.5 * math.log(k / (11.0 - k))
 
 
 def tile_kan_layer_kernel(tc, x, spline_coeffs, out):
@@ -26,31 +30,30 @@ def tile_kan_layer_kernel(tc, x, spline_coeffs, out):
     with ExitStack() as ctx:
         ctx.enter_context(nc.allow_non_contiguous_dma(reason="64-byte runs regroup the coefficients by feature class"))
         const = ctx.enter_context(tc.tile_pool(name="const", bufs=1))
-        xpp = ctx.enter_context(tc.tile_pool(name="xpp", bufs=2))
-        wgp = ctx.enter_context(tc.tile_pool(name="wgp", bufs=2))
         work = ctx.enter_context(tc.tile_pool(name="work", bufs=2))
-        idxp = ctx.enter_context(tc.tile_pool(name="idxp", bufs=3))
-        gtp = ctx.enter_context(tc.tile_pool(name="gtp", bufs=1))
-        cod = ctx.enter_context(tc.tile_pool(name="cod", bufs=4))
-        outp = ctx.enter_context(tc.tile_pool(name="outp", bufs=2))
-        psa = ctx.enter_context(tc.psum_pool(name="psa", bufs=1))
+        cod = ctx.enter_context(tc.tile_pool(name="cod", bufs=LAG + 2))
+        psa = ctx.enter_context(tc.psum_pool(name="psa", bufs=2))
+        psf = ctx.enter_context(tc.psum_pool(name="psf", bufs=2))
         psx = ctx.enter_context(tc.psum_pool(name="psx", bufs=2))
-        psw = ctx.enter_context(tc.psum_pool(name="psw", bufs=2))
 
         ident = const.tile([P, P], BF16, name="ident")
         make_identity(nc, ident[:])
+        identf = const.tile([P, P], F32, name="identf")
+        make_identity(nc, identf[:])
+        pm = const.tile([P, P, 2], BF16, name="pm")
+        nc.vector.tensor_copy(out=pm[:, :, 0], in_=ident[:])
+        nc.vector.tensor_scalar(out=pm[:, :, 1], in0=ident[:], scalar1=-1.0, scalar2=None, op0=ALU.mult)
 
-        x_sb = const.tile([P, 16, 512], BF16, name="x_sb")
-        xv = x.rearrange("(p t) i -> p t i", t=16)
-        ov = out.rearrange("(p t) o -> p t o", t=16)
+        x_sb = const.tile([P, NU, 512], BF16, name="x_sb")
+        xv = x.rearrange("(p t) i -> p t i", t=NU)
+        ov = out.rearrange("(p t) o -> p t o", t=NU)
         w_sb = [const.tile([P, 4, 1024], BF16, name="w_sb%d" % ot) for ot in range(4)]
         wv = spline_coeffs.rearrange("(ot o) (g f s) k -> ot o f g (s k)", o=P, g=32, f=4, s=4)
         w_codes = const.tile([P, 4, 2, 512], U32, name="w_codes", align_bytes=64)
         w_scales = const.tile([P, 4, 2, 512], U8, name="w_scales", align_bytes=64)
 
-
-        def load_x(c):
-            nc.sync.dma_start(out=x_sb[:, 4 * c:4 * c + 4, :], in_=xv[:, 4 * c:4 * c + 4, :])
+        def load_x(a, b):
+            nc.sync.dma_start(out=x_sb[:, a:b, :], in_=xv[:, a:b, :])
 
         def load_w(f):
             for ot in range(4):
@@ -59,65 +62,140 @@ def tile_kan_layer_kernel(tc, x, spline_coeffs, out):
                     in_=wv[ot, :, f, :, :],
                 )
 
-        load_x(0)
+        load_x(0, 2)
+        load_x(2, 4)
         load_w(0)
         load_w(1)
-        load_x(1)
+        load_x(4, 8)
         load_w(2)
         load_w(3)
-        load_x(2)
-        load_x(3)
+        load_x(8, 16)
 
         st = {}
 
-        def xperm(c):
-            xp = xpp.tile([P, 4, 512], BF16, name="xp")
-            for j in range(4):
-                (nc.vector.tensor_copy if c == 0 else nc.scalar.copy)(
-                    out=xp[:, j, :].rearrange("p (f g s) -> p f g s", f=4, g=32, s=4),
-                    in_=x_sb[:, 4 * c + j, :].rearrange("p (g f s) -> p f g s", g=32, f=4, s=4),
-                )
-            st[("xp", c)] = xp
+        def xperm(u):
+            xp = work.tile([P, 512], BF16, name="xp", bufs=3)
+            nc.vector.tensor_copy(
+                out=xp[:].rearrange("p (f g s) -> p f g s", f=4, g=32, s=4),
+                in_=x_sb[:, u, :].rearrange("p (g f s) -> p f g s", g=32, f=4, s=4),
+            )
+            st[("xp", u)] = xp
 
-        def s0(u):
-            c, f = divmod(u, 4)
-            xp = st[("xp", c)]
-            px = psx.tile([P, 512], BF16, name="px")
-            for j in range(4):
-                nc.tensor.transpose(px[:, j * P:(j + 1) * P], xp[:, j, f * P:(f + 1) * P], ident[:])
+        def sig(u):
+            xp = st[("xp", u)]
             sg = work.tile([P, 2, 512], F32, name="sg")
-            nc.scalar.activation(out=sg[:, 0, :], in_=px[:], func=ACTF.Sigmoid, scale=2.0)
-            nc.scalar.activation(out=sg[:, 1, :], in_=px[:], func=ACTF.Sigmoid, scale=-2.0)
-            idx = idxp.tile([P, 2, 2, 512], U32, name="idx")
-            nc.scalar.activation(out=idx[:, 1], in_=sg[:], func=ACTF.Copy, scale=2.75)
+            nc.scalar.activation(out=sg[:, 0, :], in_=xp[:], func=ACTF.Sigmoid, scale=2.0)
+            nc.scalar.activation(out=sg[:, 1, :], in_=xp[:], func=ACTF.Sigmoid, scale=-2.0)
             st[("sg", u)] = sg
-            st[("idx", u)] = idx
 
-        def resid(u):
-            sg = st[("sg", u)]
-            idx = st[("idx", u)]
-            pp = work.tile([P, 2, 512], F32, name="pp", bufs=3)
-            nc.vector.scalar_tensor_tensor(out=pp[:], in0=sg[:], scalar=2.75, in1=idx[:, 1].bitcast(I32), op0=ALU.mult, op1=ALU.subtract)
-            st[("pp", u)] = pp
+        def xpair(u):
+            xp = st[("xp", u)]
+            px = psx.tile([P, 4, 256], BF16, name="px")
+            for f in range(4):
+                nc.tensor.matmul(px[:, f, :], lhsT=xp[:, f * P:(f + 1) * P], rhs=pm[:].rearrange("p b s -> p (b s)"), start=True, stop=True)
+            x2 = work.tile([P, 1024], BF16, name="x2")
+            nc.scalar.copy(out=x2[:], in_=px[:].rearrange("p f n -> p (f n)"))
+            st[("x2", u)] = x2
 
-        def sq_first(u):
-            pp = st[("pp", u)]
-            nc.scalar.activation(out=pp[:], in_=pp[:], func=ACTF.Abs, scale=4.0)
-            sc = work.tile([P, 2, 512], F32, name="sc")
-            nc.scalar.activation(out=sc[:], in_=pp[:], func=ACTF.Square, scale=R23, bias=-R23)
-            st[("sc", u)] = sc
+        def uten(u):
+            ut = work.tile([P, 2, 512], F32, name="ut")
+            nc.vector.tensor_scalar(out=ut[:], in0=st[("sg", u)][:], scalar1=11.0, scalar2=10.0, op0=ALU.mult, op1=ALU.min)
+            st[("ut", u)] = ut
 
-        def sq_rest(u):
-            pp = st[("pp", u)]
-            sa = work.tile([P, 2, 512], F32, name="sa")
-            sb = work.tile([P, 2, 512], F32, name="sb")
-            nc.scalar.activation(out=sa[:], in_=pp[:], func=ACTF.Square, scale=R6)
-            nc.scalar.activation(out=sb[:], in_=pp[:], func=ACTF.Square, scale=-R6, bias=2.0 * R6)
-            nc.scalar.activation(out=st[("idx", u)][:, 0], in_=st[("sg", u)][:], func=ACTF.Copy, scale=2.75, bias=0.5)
-            st[("sab", u)] = (sa, sb)
+        def folds(u):
+            fh = work.tile([P, 2, 512], F32, name="fh")
+            nc.scalar.activation(out=fh[:], in_=st[("ut", u)][:], func=ACTF.Abs, bias=-7.0)
+            nc.scalar.activation(out=fh[:], in_=fh[:], func=ACTF.Abs, bias=-2.0)
+            nc.scalar.activation(out=fh[:], in_=fh[:], func=ACTF.Abs, bias=-2.0)
+            st[("fh", u)] = fh
+
+        def wave(u):
+            z = work.tile([P, 2, 512], F32, name="z")
+            nc.vector.scalar_tensor_tensor(out=z[:], in0=st[("fh", u)][:], scalar=-1.0, in1=st[("ut", u)][:], op0=ALU.add, op1=ALU.min)
+            st[("z", u)] = z
+
+        def square(u):
+            q = work.tile([P, 2, 512], F32, name="q")
+            nc.scalar.activation(out=q[:], in_=st[("z", u)][:], func=ACTF.Square, scale=1.0 / math.sqrt(3.0))
+            st[("q", u)] = q
+
+        def cube(u):
+            y = work.tile([P, 2, 512], F32, name="y")
+            nc.vector.scalar_tensor_tensor(out=y[:], in0=st[("z", u)][:], scalar=-1.0, in1=st[("q", u)][:], op0=ALU.mult, op1=ALU.mult)
+            st[("y", u)] = y
+
+        def masks(u):
+            x2 = st[("x2", u)]
+            m1 = work.tile([P, 2, 1024], BF16, name="m1")
+            m2 = work.tile([P, 2, 1024], BF16, name="m2")
+            nc.vector.tensor_scalar(out=m1[:, 0, :], in0=x2[:], scalar1=knot_x(4), scalar2=None, op0=ALU.is_lt)
+            nc.vector.tensor_scalar(out=m1[:, 1, :], in0=x2[:], scalar1=knot_x(6), scalar2=None, op0=ALU.is_gt)
+            nc.vector.tensor_scalar(out=m2[:, 0, :], in0=x2[:], scalar1=knot_x(8), scalar2=None, op0=ALU.is_lt)
+            nc.vector.tensor_scalar(out=m2[:, 1, :], in0=x2[:], scalar1=knot_x(2), scalar2=None, op0=ALU.is_gt)
+            st[("m", u)] = (m1, m2)
+
+        def turn(u, h):
+            z = st[("z", u)]
+            y = st[("y", u)]
+            yt = psf.tile([P, 2, 256], F32, name="yt")
+            wt = psf.tile([P, 2, 256], F32, name="wt")
+            for s in range(2):
+                for e in range(2):
+                    cols = slice((2 * h + e) * P, (2 * h + e + 1) * P)
+                    dst = slice(e * P, (e + 1) * P)
+                    nc.tensor.matmul(yt[:, s, dst], lhsT=y[:, s, cols], rhs=identf[:], is_transpose=True, start=True, stop=True)
+                    nc.tensor.matmul(wt[:, s, dst], lhsT=z[:, 1 - s, cols], rhs=identf[:], is_transpose=True, start=True, stop=False)
+                    nc.tensor.matmul(wt[:, s, dst], lhsT=y[:, 1 - s, cols], rhs=identf[:], is_transpose=True, start=False, stop=True)
+            st[("t", u, h)] = (yt, wt)
+
+        def small(u, h):
+            yt, wt = st[("t", u, h)]
+            sm = work.tile([P, 256, 2], F32, name="sm")
+            nc.scalar.activation(out=sm[:], in_=yt[:].rearrange("p s b -> p b s"), func=ACTF.Abs, scale=0.5)
+            st[("sm", u, h)] = sm
+
+        def combine(u, h):
+            if h == 0:
+                st[("cv", u)] = work.tile([P, 2, 1024], BF16, name="cv")
+            cv = st[("cv", u)]
+            yt, wt = st[("t", u, h)]
+            sm = st[("sm", u, h)]
+            cols = slice(512 * h, 512 * h + 512)
+            wv2 = wt[:].rearrange("p s b -> p b s")
+            nc.vector.scalar_tensor_tensor(out=cv[:, 0, cols].rearrange("p (b s) -> p b s", s=2), in0=wv2, scalar=0.0, in1=sm[:], op0=ALU.max, op1=ALU.add)
+            nc.vector.scalar_tensor_tensor(out=cv[:, 1, cols].rearrange("p (b s) -> p b s", s=2), in0=wv2, scalar=0.0, in1=sm[:], op0=ALU.min, op1=ALU.subtract, reverse1=True)
+
+        def gate_first(u):
+            cv = st[("cv", u)]
+            m1, m2 = st[("m", u)]
+            g0 = work.tile([P, 512, 2, 2], BF16, name="g0", align_bytes=64)
+            nc.vector.tensor_tensor(
+                out=g0[:],
+                in0=cv[:].rearrange("p v (b s) -> p b v s", s=2),
+                in1=m1[:].rearrange("p v (b s) -> p b v s", s=2),
+                op=ALU.mult,
+            )
+            st[("g", u, 0)] = g0
+
+        def gate_alive(u):
+            cv = st[("cv", u)]
+            m1, m2 = st[("m", u)]
+            al = work.tile([P, 2, 1024], BF16, name="al")
+            nc.vector.tensor_tensor(out=al[:], in0=cv[:], in1=m2[:], op=ALU.mult)
+            st[("al", u)] = al
+
+        def gate_second(u):
+            g1 = work.tile([P, 512, 2, 2], BF16, name="g1", align_bytes=64)
+            nc.vector.tensor_tensor(
+                out=g1[:],
+                in0=st[("al", u)][:].rearrange("p v (b s) -> p b v s", s=2),
+                in1=st[("g", u, 0)][:],
+                op=ALU.subtract,
+            )
+            st[("g", u, 1)] = g1
 
         def quant(u, ps):
-            if ("codes", u) not in st:
+            if ps == 0:
                 codes = cod.tile([P, 2, 512], U32, name="codes", align_bytes=64)
                 scl = cod.tile([P, 2, 512], U8, name="scl", align_bytes=64)
                 st[("codes", u)] = (codes, scl)
@@ -125,149 +203,87 @@ def tile_kan_layer_kernel(tc, x, spline_coeffs, out):
             nc.vector.quantize_mx(
                 out=codes[:, ps, :].bitcast(FP8X4),
                 scales=scl[:, ps, :],
-                in_=st[("gt", u, ps)][:].rearrange("p b t -> p (b t)"),
+                in_=st[("g", u, ps)][:].rearrange("p b v s -> p (b v s)"),
             )
 
-        def products(u):
-            pp = st[("pp", u)]
-            sc = st[("sc", u)]
-            sa, sb = st[("sab", u)]
-            nc.vector.scalar_tensor_tensor(out=sc[:], in0=pp[:], scalar=-1.0, in1=sc[:], op0=ALU.add, op1=ALU.mult)
-            nc.vector.tensor_tensor(out=sa[:], in0=pp[:], in1=sa[:], op=ALU.mult)
-            nc.vector.scalar_tensor_tensor(out=sb[:], in0=pp[:], scalar=-2.0, in1=sb[:], op0=ALU.add, op1=ALU.mult)
-
-        def combine(u):
-            sc = st[("sc", u)]
-            sa, sb = st[("sab", u)]
-            cv = work.tile([P, 2, 2, 512], BF16, name="cv")
-            nc.vector.scalar_tensor_tensor(out=cv[:, 0], in0=sc[:], scalar=0.0, in1=sa[:], op0=ALU.max, op1=ALU.subtract, reverse1=True)
-            nc.vector.scalar_tensor_tensor(out=cv[:, 1], in0=sc[:], scalar=0.0, in1=sb[:], op0=ALU.min, op1=ALU.subtract)
-            st[("cv", u)] = cv
-
-        def gate_planes(u):
-            gpl = gtp.tile([P, 4, 512], BF16, name="gpl")
-            nc.vector.scalar_tensor_tensor(
-                out=gpl[:].rearrange("p t b -> p (t b)"),
-                in0=st[("idx", u)][:].bitcast(I32).rearrange("p v s b -> p (v s b)"),
-                scalar=1.0,
-                in1=st[("cv", u)][:].rearrange("p v s b -> p (v s b)"),
-                op0=ALU.is_equal,
-                op1=ALU.mult,
-            )
-            st[("gpl", u)] = gpl
-
-        def weave(u):
-            gt = gtp.tile([P, 512, 4], BF16, name="gt0", align_bytes=64)
-            nc.scalar.copy(out=gt[:], in_=st[("gpl", u)][:].rearrange("p t b -> p b t"))
-            st[("gt", u, 0)] = gt
-
-        def gate_woven(u, ps):
-            gt = gtp.tile([P, 512, 4], BF16, name="gt%d" % ps, align_bytes=64)
-            nc.vector.scalar_tensor_tensor(
-                out=gt[:],
-                in0=st[("idx", u)][:].bitcast(I32).rearrange("p v s b -> p b (v s)"),
-                scalar=float(ps + 1),
-                in1=st[("cv", u)][:].rearrange("p v s b -> p b (v s)"),
-                op0=ALU.is_equal,
-                op1=ALU.mult,
-            )
-            st[("gt", u, ps)] = gt
-
-        def prep_w_move(f):
-            wgs = []
-            for ps in range(2):
-                wg = wgp.tile([P, 512, 4], BF16, name="wg", align_bytes=64)
-                for ot in range(4):
-                    pw = psw.tile([P, 4, P], BF16, name="pw")
-                    wk = w_sb[ot][:, f, :].rearrange("o (j k) -> o j k", k=8)
+        def prep_w_move(f, ps):
+            wg = work.tile([P, 512, 4], BF16, name="wg", align_bytes=64)
+            for h in range(2):
+                pw = psx.tile([P, 4, 256], BF16, name="px")
+                for e in range(2):
+                    wk = w_sb[2 * h + e][:, f, :].rearrange("o (j k) -> o j k", k=8)
                     for t in range(4):
-                        nc.tensor.transpose(pw[:, t, :], wk[:, :, SLOT[ps][t]], ident[:])
-                    nc.scalar.copy(out=wg[:, ot * P:(ot + 1) * P, :], in_=pw[:].rearrange("p t o -> p o t"))
-                wgs.append(wg)
-            st[("wg", f)] = wgs
+                        nc.tensor.transpose(pw[:, t, e * P:(e + 1) * P], wk[:, :, SLOT[ps][t]], ident[:])
+                nc.scalar.copy(out=wg[:, h * 256:(h + 1) * 256, :], in_=pw[:].rearrange("p t o -> p o t"))
+            st[("wg", f, ps)] = wg
 
-        def prep_w_quant(f):
-            for ps in range(2):
-                nc.vector.quantize_mx(
-                    out=w_codes[:, f, ps, :].bitcast(FP8X4),
-                    scales=w_scales[:, f, ps, :],
-                    in_=st[("wg", f)][ps][:].rearrange("p o t -> p (o t)"),
-                )
+        def prep_w_quant(f, ps):
+            nc.vector.quantize_mx(
+                out=w_codes[:, f, ps, :].bitcast(FP8X4),
+                scales=w_scales[:, f, ps, :],
+                in_=st[("wg", f, ps)][:].rearrange("p o t -> p (o t)"),
+            )
 
         def mm(u):
-            c, f = divmod(u, 4)
-            if f == 0:
-                st[("acc", c)] = [psa.tile([P, 512], F32, name="acc%d" % j) for j in range(4)]
-            acc = st[("acc", c)]
+            acc = psa.tile([P, 512], F32, name="acc")
             codes, scl = st[("codes", u)]
+            n = 0
             for ps in range(2):
-                for j in range(4):
+                for f in range(4):
                     nc.tensor.matmul_mx(
-                        out=acc[j][:],
-                        lhsT=codes[:, ps, j * P:(j + 1) * P].bitcast(FP8X4),
-                        lhsT_scale=scl[:, ps, j * P:(j + 1) * P],
+                        out=acc[:],
+                        lhsT=codes[:, ps, f * P:(f + 1) * P].bitcast(FP8X4),
+                        lhsT_scale=scl[:, ps, f * P:(f + 1) * P],
                         rhs=w_codes[:, f, ps, :].bitcast(FP8X4),
                         rhs_scale=w_scales[:, f, ps, :],
-                        start=(f == 0 and ps == 0),
-                        stop=(f == 3 and ps == 1),
+                        start=(n == 0),
+                        stop=(n == 7),
                     )
+                    n += 1
+            osb = work.tile([P, 512], F32, name="osb")
+            nc.scalar.copy(out=osb[:], in_=acc[:])
+            nc.sync.dma_start(out=ov[:, u, :], in_=osb[:])
 
-        def evac(c):
-            acc = st[("acc", c)]
-            osb = outp.tile([P, 4, 512], F32, name="osb")
-            if c < 3:
-                for j in range(4):
-                    nc.scalar.copy(out=osb[:, j, :], in_=acc[j][:])
-                nc.sync.dma_start(out=ov[:, 4 * c:4 * c + 4, :], in_=osb[:])
-            else:
-                for h in range(2):
-                    nc.scalar.copy(out=osb[:, 2 * h, :], in_=acc[2 * h][:])
-                    nc.vector.tensor_copy(out=osb[:, 2 * h + 1, :], in_=acc[2 * h + 1][:])
-                    nc.sync.dma_start(out=ov[:, 4 * c + 2 * h:4 * c + 2 * h + 2, :], in_=osb[:, 2 * h:2 * h + 2, :])
+        def ok(u):
+            return 0 <= u < NU
 
-        NU = 16
-        LAG = 2
-        xperm(0)
-        s0(0)
-        resid(0)
-        sq_first(0)
-        sq_rest(0)
-        s0(1)
-        resid(1)
-        for i in range(NU + LAG):
-            if 1 <= i < NU:
-                weave(i - 1)
-            if i + 2 < NU:
-                if (i + 2) % 4 == 0:
-                    xperm((i + 2) // 4)
-                s0(i + 2)
-            if i + 1 < NU:
-                sq_first(i + 1)
-                sq_rest(i + 1)
-            m = i - LAG
-            if m > 0 and m % 4 == 0:
-                evac(m // 4 - 1)
-            if 0 <= m < 4:
-                prep_w_move(m)
-            if i < NU:
-                products(i)
-            if 1 <= i <= NU:
-                quant(i - 1, 1)
-            if i < NU:
-                combine(i)
-            if i + 2 < NU:
-                resid(i + 2)
-            if i < NU - 1:
-                gate_planes(i)
-            if i == NU - 1:
-                quant(i - 1, 0)
-                gate_woven(i, 0)
-            if i < NU:
-                gate_woven(i, 1)
-            if 1 <= i <= NU and i != NU - 1:
-                quant(i - 1, 0)
-            if 0 <= m < 4:
-                prep_w_quant(m)
-            if m >= 0:
-                mm(m)
-        evac(3)
+        for i in range(-1, NU + LAG + 2):
+            a = i - 2
+            if ok(a):
+                turn(a, 0)
+                small(a, 0)
+                turn(a, 1)
+                small(a, 1)
+            if ok(i - 1):
+                wave(i - 1)
+            if ok(a):
+                combine(a, 0)
+            if ok(i - 1):
+                square(i - 1)
+                cube(i - 1)
+            if ok(a):
+                combine(a, 1)
+            if ok(i + 1):
+                xperm(i + 1)
+                sig(i + 1)
+            if ok(i):
+                folds(i)
+                xpair(i)
+            if ok(i - 1):
+                masks(i - 1)
+            if ok(a):
+                gate_first(a)
+                gate_alive(a)
+            if ok(i + 1):
+                uten(i + 1)
+            if ok(a):
+                gate_second(a)
+                quant(a, 0)
+            if WSTEP <= i < WSTEP + 4:
+                for ps in range(2):
+                    prep_w_move(i - WSTEP, ps)
+                    prep_w_quant(i - WSTEP, ps)
+            if ok(a):
+                quant(a, 1)
+            if ok(a - LAG):
+                mm(a - LAG)

@@ -16,7 +16,7 @@ ACTF = mybir.ActivationFunctionType
 
 P = 128
 NU = 16
-LAG = 3
+LAG = 2
 WSTEP = 1
 SLOT = ((0, 7, 6, 1), (4, 3, 2, 5))
 
@@ -31,7 +31,7 @@ def tile_kan_layer_kernel(tc, x, spline_coeffs, out):
         ctx.enter_context(nc.allow_non_contiguous_dma(reason="64-byte runs regroup the coefficients by feature class"))
         const = ctx.enter_context(tc.tile_pool(name="const", bufs=1))
         work = ctx.enter_context(tc.tile_pool(name="work", bufs=2))
-        cod = ctx.enter_context(tc.tile_pool(name="cod", bufs=LAG + 2))
+        cod = ctx.enter_context(tc.tile_pool(name="cod", bufs=LAG + 3))
         psa = ctx.enter_context(tc.psum_pool(name="psa", bufs=2))
         psf = ctx.enter_context(tc.psum_pool(name="psf", bufs=2))
         psx = ctx.enter_context(tc.psum_pool(name="psx", bufs=2))
@@ -62,14 +62,12 @@ def tile_kan_layer_kernel(tc, x, spline_coeffs, out):
                     in_=wv[ot, :, f, :, :],
                 )
 
-        load_x(0, 2)
-        load_x(2, 4)
-        load_w(0)
-        load_w(1)
+        load_x(0, 1)
+        load_x(1, 4)
         load_x(4, 8)
-        load_w(2)
-        load_w(3)
         load_x(8, 16)
+        for f in range(4):
+            load_w(f)
 
         st = {}
 
@@ -247,43 +245,47 @@ def tile_kan_layer_kernel(tc, x, spline_coeffs, out):
         def ok(u):
             return 0 <= u < NU
 
-        for i in range(-1, NU + LAG + 2):
+        for i in range(-2, NU + LAG + 3):
             a = i - 2
+            b = i - 3
             if ok(a):
-                turn(a, 0)
                 small(a, 0)
-                turn(a, 1)
                 small(a, 1)
+                combine(a, 0)
+            if ok(i):
+                folds(i)
+                xpair(i)
+            if ok(b):
+                gate_second(b)
+            if ok(a):
+                combine(a, 1)
+            if ok(b):
+                quant(b, 0)
             if ok(i - 1):
                 wave(i - 1)
             if ok(a):
-                combine(a, 0)
+                gate_first(a)
             if ok(i - 1):
                 square(i - 1)
                 cube(i - 1)
             if ok(a):
-                combine(a, 1)
+                gate_alive(a)
+            if ok(b):
+                quant(b, 1)
+            if ok(i - 1):
+                turn(i - 1, 0)
+                turn(i - 1, 1)
             if ok(i + 1):
-                xperm(i + 1)
                 sig(i + 1)
-            if ok(i):
-                folds(i)
-                xpair(i)
             if ok(i - 1):
                 masks(i - 1)
-            if ok(a):
-                gate_first(a)
-                gate_alive(a)
-            if ok(i + 1):
-                uten(i + 1)
-            if ok(a):
-                gate_second(a)
-                quant(a, 0)
             if WSTEP <= i < WSTEP + 4:
                 for ps in range(2):
                     prep_w_move(i - WSTEP, ps)
                     prep_w_quant(i - WSTEP, ps)
-            if ok(a):
-                quant(a, 1)
-            if ok(a - LAG):
-                mm(a - LAG)
+            if ok(i + 1):
+                uten(i + 1)
+            if ok(i + 2):
+                xperm(i + 2)
+            if ok(b - LAG):
+                mm(b - LAG)

@@ -16,8 +16,9 @@ ACTF = mybir.ActivationFunctionType
 
 P = 128
 NU = 16
-LAG = 2
 WSTEP = 1
+MID_A = 54.0 / 512.0
+HALF_A = 197.5 / 512.0
 SLOT = ((0, 7, 6, 1), (4, 3, 2, 5))
 
 
@@ -31,7 +32,7 @@ def tile_kan_layer_kernel(tc, x, spline_coeffs, out):
         ctx.enter_context(nc.allow_non_contiguous_dma(reason="64-byte runs regroup the coefficients by feature class"))
         const = ctx.enter_context(tc.tile_pool(name="const", bufs=1))
         work = ctx.enter_context(tc.tile_pool(name="work", bufs=2))
-        cod = ctx.enter_context(tc.tile_pool(name="cod", bufs=LAG + 3))
+        cod = ctx.enter_context(tc.tile_pool(name="cod", bufs=WSTEP + 8))
         psa = ctx.enter_context(tc.psum_pool(name="psa", bufs=2))
         psf = ctx.enter_context(tc.psum_pool(name="psf", bufs=2))
         psx = ctx.enter_context(tc.psum_pool(name="psx", bufs=2))
@@ -93,7 +94,10 @@ def tile_kan_layer_kernel(tc, x, spline_coeffs, out):
                 nc.tensor.matmul(px[:, f, :], lhsT=xp[:, f * P:(f + 1) * P], rhs=pm[:].rearrange("p b s -> p (b s)"), start=True, stop=True)
             x2 = work.tile([P, 1024], BF16, name="x2")
             nc.scalar.copy(out=x2[:], in_=px[:].rearrange("p f n -> p (f n)"))
+            xd = work.tile([P, 1024], BF16, name="xd")
+            nc.scalar.activation(out=xd[:], in_=px[:].rearrange("p f n -> p (f n)"), func=ACTF.Abs, bias=-MID_A)
             st[("x2", u)] = x2
+            st[("xd", u)] = xd
 
         def uten(u):
             ut = work.tile([P, 2, 512], F32, name="ut")
@@ -118,19 +122,21 @@ def tile_kan_layer_kernel(tc, x, spline_coeffs, out):
             st[("q", u)] = q
 
         def cube(u):
-            y = work.tile([P, 2, 512], F32, name="y")
-            nc.vector.scalar_tensor_tensor(out=y[:], in0=st[("z", u)][:], scalar=-1.0, in1=st[("q", u)][:], op0=ALU.mult, op1=ALU.mult)
-            st[("y", u)] = y
+            q = st[("q", u)]
+            nc.vector.scalar_tensor_tensor(out=q[:], in0=st[("z", u)][:], scalar=-1.0, in1=q[:], op0=ALU.mult, op1=ALU.mult)
+            st[("y", u)] = q
 
         def masks(u):
             x2 = st[("x2", u)]
             m1 = work.tile([P, 2, 1024], BF16, name="m1")
-            m2 = work.tile([P, 2, 1024], BF16, name="m2")
+            m2 = work.tile([P, 1024], BF16, name="m2")
+            mb = work.tile([P, 2, 1024], BF16, name="mb")
             nc.vector.tensor_scalar(out=m1[:, 0, :], in0=x2[:], scalar1=knot_x(4), scalar2=None, op0=ALU.is_lt)
             nc.vector.tensor_scalar(out=m1[:, 1, :], in0=x2[:], scalar1=knot_x(6), scalar2=None, op0=ALU.is_gt)
-            nc.vector.tensor_scalar(out=m2[:, 0, :], in0=x2[:], scalar1=knot_x(8), scalar2=None, op0=ALU.is_lt)
-            nc.vector.tensor_scalar(out=m2[:, 1, :], in0=x2[:], scalar1=knot_x(2), scalar2=None, op0=ALU.is_gt)
-            st[("m", u)] = (m1, m2)
+            nc.vector.tensor_scalar(out=m2[:], in0=x2[:], scalar1=knot_x(2), scalar2=None, op0=ALU.is_gt)
+            nc.vector.tensor_scalar(out=mb[:, 0, :], in0=st[("xd", u)][:], scalar1=HALF_A, scalar2=None, op0=ALU.is_lt)
+            nc.vector.tensor_tensor(out=mb[:, 1, :], in0=m2[:], in1=m1[:, 1, :], op=ALU.subtract)
+            st[("m", u)] = (m1, mb)
 
         def turn(u, h):
             z = st[("z", u)]
@@ -165,7 +171,7 @@ def tile_kan_layer_kernel(tc, x, spline_coeffs, out):
 
         def gate_first(u):
             cv = st[("cv", u)]
-            m1, m2 = st[("m", u)]
+            m1, mb = st[("m", u)]
             g0 = work.tile([P, 512, 2, 2], BF16, name="g0", align_bytes=64)
             nc.vector.tensor_tensor(
                 out=g0[:],
@@ -175,20 +181,15 @@ def tile_kan_layer_kernel(tc, x, spline_coeffs, out):
             )
             st[("g", u, 0)] = g0
 
-        def gate_alive(u):
-            cv = st[("cv", u)]
-            m1, m2 = st[("m", u)]
-            al = work.tile([P, 2, 1024], BF16, name="al")
-            nc.vector.tensor_tensor(out=al[:], in0=cv[:], in1=m2[:], op=ALU.mult)
-            st[("al", u)] = al
-
         def gate_second(u):
+            cv = st[("cv", u)]
+            m1, mb = st[("m", u)]
             g1 = work.tile([P, 512, 2, 2], BF16, name="g1", align_bytes=64)
             nc.vector.tensor_tensor(
                 out=g1[:],
-                in0=st[("al", u)][:].rearrange("p v (b s) -> p b v s", s=2),
-                in1=st[("g", u, 0)][:],
-                op=ALU.subtract,
+                in0=cv[:].rearrange("p v (b s) -> p b v s", s=2),
+                in1=mb[:].rearrange("p v (b s) -> p b v s", s=2),
+                op=ALU.mult,
             )
             st[("g", u, 1)] = g1
 
@@ -245,47 +246,48 @@ def tile_kan_layer_kernel(tc, x, spline_coeffs, out):
         def ok(u):
             return 0 <= u < NU
 
-        for i in range(-2, NU + LAG + 3):
+        done = 0
+        for i in range(-2, NU + 4):
             a = i - 2
             b = i - 3
             if ok(a):
                 small(a, 0)
                 small(a, 1)
                 combine(a, 0)
-            if ok(i):
-                folds(i)
-                xpair(i)
-            if ok(b):
-                gate_second(b)
+            if ok(i - 1):
+                wave(i - 1)
+                square(i - 1)
             if ok(a):
+                masks(a)
                 combine(a, 1)
             if ok(b):
                 quant(b, 0)
             if ok(i - 1):
-                wave(i - 1)
-            if ok(a):
-                gate_first(a)
-            if ok(i - 1):
-                square(i - 1)
                 cube(i - 1)
-            if ok(a):
-                gate_alive(a)
-            if ok(b):
-                quant(b, 1)
-            if ok(i - 1):
                 turn(i - 1, 0)
                 turn(i - 1, 1)
+            if ok(i):
+                folds(i)
+            if ok(a):
+                gate_first(a)
+            if ok(b):
+                quant(b, 1)
+            if ok(a):
+                gate_second(a)
             if ok(i + 1):
                 sig(i + 1)
             if ok(i - 1):
-                masks(i - 1)
-            if WSTEP <= i < WSTEP + 4:
-                for ps in range(2):
-                    prep_w_move(i - WSTEP, ps)
-                    prep_w_quant(i - WSTEP, ps)
+                xpair(i - 1)
+            if WSTEP <= i < WSTEP + 8:
+                prep_w_move((i - WSTEP) // 2, (i - WSTEP) % 2)
             if ok(i + 1):
                 uten(i + 1)
+            if WSTEP <= i < WSTEP + 8:
+                prep_w_quant((i - WSTEP) // 2, (i - WSTEP) % 2)
             if ok(i + 2):
                 xperm(i + 2)
-            if ok(b - LAG):
-                mm(b - LAG)
+            if i >= WSTEP + 7:
+                for n in range(2):
+                    if done <= b and done < NU:
+                        mm(done)
+                        done += 1

@@ -17,8 +17,11 @@ ACTF = mybir.ActivationFunctionType
 P = 128
 NU = 16
 WSTEP = 1
+WSPAN = 11
 MID_A = 54.0 / 512.0
 HALF_A = 197.5 / 512.0
+FULL = slice(0, 512)
+HALVES = (slice(0, 256), slice(256, 512))
 SLOT = ((0, 7, 6, 1), (4, 3, 2, 5))
 
 
@@ -32,7 +35,7 @@ def tile_kan_layer_kernel(tc, x, spline_coeffs, out):
         ctx.enter_context(nc.allow_non_contiguous_dma(reason="64-byte runs regroup the coefficients by feature class"))
         const = ctx.enter_context(tc.tile_pool(name="const", bufs=1))
         work = ctx.enter_context(tc.tile_pool(name="work", bufs=2))
-        cod = ctx.enter_context(tc.tile_pool(name="cod", bufs=WSTEP + 8))
+        cod = ctx.enter_context(tc.tile_pool(name="cod", bufs=WSTEP + WSPAN))
         psa = ctx.enter_context(tc.psum_pool(name="psa", bufs=2))
         psf = ctx.enter_context(tc.psum_pool(name="psf", bufs=2))
         psx = ctx.enter_context(tc.psum_pool(name="psx", bufs=2))
@@ -45,7 +48,6 @@ def tile_kan_layer_kernel(tc, x, spline_coeffs, out):
         nc.vector.tensor_copy(out=pm[:, :, 0], in_=ident[:])
         nc.vector.tensor_scalar(out=pm[:, :, 1], in0=ident[:], scalar1=-1.0, scalar2=None, op0=ALU.mult)
 
-        x_sb = const.tile([P, NU, 512], BF16, name="x_sb")
         xv = x.rearrange("(p t) i -> p t i", t=NU)
         ov = out.rearrange("(p t) o -> p t o", t=NU)
         w_sb = [const.tile([P, 4, 1024], BF16, name="w_sb%d" % ot) for ot in range(4)]
@@ -53,8 +55,16 @@ def tile_kan_layer_kernel(tc, x, spline_coeffs, out):
         w_codes = const.tile([P, 4, 2, 512], U32, name="w_codes", align_bytes=64)
         w_scales = const.tile([P, 4, 2, 512], U8, name="w_scales", align_bytes=64)
 
-        def load_x(a, b):
-            nc.sync.dma_start(out=x_sb[:, a:b, :], in_=xv[:, a:b, :])
+        st = {}
+
+        def load_x(c):
+            xc = work.tile([P, 4, 512], BF16, name="xc")
+            if c == 0:
+                nc.sync.dma_start(out=xc[:, 0:1, :], in_=xv[:, 0:1, :])
+                nc.sync.dma_start(out=xc[:, 1:4, :], in_=xv[:, 1:4, :])
+            else:
+                nc.sync.dma_start(out=xc[:], in_=xv[:, 4 * c:4 * c + 4, :])
+            st[("xc", c)] = xc
 
         def load_w(f):
             for ot in range(4):
@@ -63,29 +73,29 @@ def tile_kan_layer_kernel(tc, x, spline_coeffs, out):
                     in_=wv[ot, :, f, :, :],
                 )
 
-        load_x(0, 1)
-        load_x(1, 4)
-        load_x(4, 8)
-        load_x(8, 16)
+        load_x(0)
+        load_x(1)
         for f in range(4):
             load_w(f)
-
-        st = {}
 
         def xperm(u):
             xp = work.tile([P, 512], BF16, name="xp", bufs=3)
             nc.vector.tensor_copy(
                 out=xp[:].rearrange("p (f g s) -> p f g s", f=4, g=32, s=4),
-                in_=x_sb[:, u, :].rearrange("p (g f s) -> p f g s", g=32, f=4, s=4),
+                in_=st[("xc", u // 4)][:, u % 4, :].rearrange("p (g f s) -> p f g s", g=32, f=4, s=4),
             )
             st[("xp", u)] = xp
 
-        def sig(u):
+        def tile_of(key, u, shape, dtype, **kw):
+            if (key, u) not in st:
+                st[(key, u)] = work.tile(shape, dtype, name=key, **kw)
+            return st[(key, u)]
+
+        def sig(u, c=FULL):
             xp = st[("xp", u)]
-            sg = work.tile([P, 2, 512], F32, name="sg")
-            nc.scalar.activation(out=sg[:, 0, :], in_=xp[:], func=ACTF.Sigmoid, scale=2.0)
-            nc.scalar.activation(out=sg[:, 1, :], in_=xp[:], func=ACTF.Sigmoid, scale=-2.0)
-            st[("sg", u)] = sg
+            sg = tile_of("sg", u, [P, 2, 512], F32, bufs=3)
+            nc.scalar.activation(out=sg[:, 0, c], in_=xp[:, c], func=ACTF.Sigmoid, scale=2.0)
+            nc.scalar.activation(out=sg[:, 1, c], in_=xp[:, c], func=ACTF.Sigmoid, scale=-2.0)
 
         def xpair(u):
             xp = st[("xp", u)]
@@ -99,32 +109,27 @@ def tile_kan_layer_kernel(tc, x, spline_coeffs, out):
             st[("x2", u)] = x2
             st[("xd", u)] = xd
 
-        def uten(u):
-            ut = work.tile([P, 2, 512], F32, name="ut")
-            nc.vector.tensor_scalar(out=ut[:], in0=st[("sg", u)][:], scalar1=11.0, scalar2=10.0, op0=ALU.mult, op1=ALU.min)
-            st[("ut", u)] = ut
+        def uten(u, c=FULL):
+            sg = st[("sg", u)]
+            nc.vector.tensor_scalar(out=sg[:, :, c], in0=sg[:, :, c], scalar1=11.0, scalar2=10.0, op0=ALU.mult, op1=ALU.min)
 
-        def folds(u):
-            fh = work.tile([P, 2, 512], F32, name="fh")
-            nc.scalar.activation(out=fh[:], in_=st[("ut", u)][:], func=ACTF.Abs, bias=-7.0)
-            nc.scalar.activation(out=fh[:], in_=fh[:], func=ACTF.Abs, bias=-2.0)
-            nc.scalar.activation(out=fh[:], in_=fh[:], func=ACTF.Abs, bias=-2.0)
-            st[("fh", u)] = fh
+        def folds(u, c=FULL):
+            fh = tile_of("fh", u, [P, 2, 512], F32)
+            nc.scalar.activation(out=fh[:, :, c], in_=st[("sg", u)][:, :, c], func=ACTF.Abs, bias=-7.0)
+            nc.scalar.activation(out=fh[:, :, c], in_=fh[:, :, c], func=ACTF.Abs, bias=-2.0)
+            nc.scalar.activation(out=fh[:, :, c], in_=fh[:, :, c], func=ACTF.Abs, bias=-2.0)
 
-        def wave(u):
-            z = work.tile([P, 2, 512], F32, name="z")
-            nc.vector.scalar_tensor_tensor(out=z[:], in0=st[("fh", u)][:], scalar=-1.0, in1=st[("ut", u)][:], op0=ALU.add, op1=ALU.min)
-            st[("z", u)] = z
+        def wave(u, c=FULL):
+            z = tile_of("z", u, [P, 2, 512], F32)
+            nc.vector.scalar_tensor_tensor(out=z[:, :, c], in0=st[("fh", u)][:, :, c], scalar=-1.0, in1=st[("sg", u)][:, :, c], op0=ALU.add, op1=ALU.min)
 
-        def square(u):
-            q = work.tile([P, 2, 512], F32, name="q")
-            nc.scalar.activation(out=q[:], in_=st[("z", u)][:], func=ACTF.Square, scale=1.0 / math.sqrt(3.0))
-            st[("q", u)] = q
+        def square(u, c=FULL):
+            q = tile_of("q", u, [P, 2, 512], F32)
+            nc.scalar.activation(out=q[:, :, c], in_=st[("z", u)][:, :, c], func=ACTF.Square, scale=1.0 / math.sqrt(3.0))
 
-        def cube(u):
+        def cube(u, c=FULL):
             q = st[("q", u)]
-            nc.vector.scalar_tensor_tensor(out=q[:], in0=st[("z", u)][:], scalar=-1.0, in1=q[:], op0=ALU.mult, op1=ALU.mult)
-            st[("y", u)] = q
+            nc.vector.scalar_tensor_tensor(out=q[:, :, c], in0=st[("z", u)][:, :, c], scalar=-1.0, in1=q[:, :, c], op0=ALU.mult, op1=ALU.mult)
 
         def masks(u):
             x2 = st[("x2", u)]
@@ -140,7 +145,7 @@ def tile_kan_layer_kernel(tc, x, spline_coeffs, out):
 
         def turn(u, h):
             z = st[("z", u)]
-            y = st[("y", u)]
+            y = st[("q", u)]
             yt = psf.tile([P, 2, 256], F32, name="yt")
             wt = psf.tile([P, 2, 256], F32, name="wt")
             for s in range(2):
@@ -169,52 +174,39 @@ def tile_kan_layer_kernel(tc, x, spline_coeffs, out):
             nc.vector.scalar_tensor_tensor(out=cv[:, 0, cols].rearrange("p (b s) -> p b s", s=2), in0=wv2, scalar=0.0, in1=sm[:], op0=ALU.max, op1=ALU.add)
             nc.vector.scalar_tensor_tensor(out=cv[:, 1, cols].rearrange("p (b s) -> p b s", s=2), in0=wv2, scalar=0.0, in1=sm[:], op0=ALU.min, op1=ALU.subtract, reverse1=True)
 
-        def gate_first(u):
+        def gate(u, ps, c=FULL):
             cv = st[("cv", u)]
-            m1, mb = st[("m", u)]
-            g0 = work.tile([P, 512, 2, 2], BF16, name="g0", align_bytes=64)
+            g = tile_of("g%d" % ps, u, [P, 512, 2, 2], BF16, align_bytes=64)
+            pairs = slice(2 * c.start, 2 * c.stop)
             nc.vector.tensor_tensor(
-                out=g0[:],
-                in0=cv[:].rearrange("p v (b s) -> p b v s", s=2),
-                in1=m1[:].rearrange("p v (b s) -> p b v s", s=2),
+                out=g[:, c],
+                in0=cv[:, :, pairs].rearrange("p v (b s) -> p b v s", s=2),
+                in1=st[("m", u)][ps][:, :, pairs].rearrange("p v (b s) -> p b v s", s=2),
                 op=ALU.mult,
             )
-            st[("g", u, 0)] = g0
 
-        def gate_second(u):
-            cv = st[("cv", u)]
-            m1, mb = st[("m", u)]
-            g1 = work.tile([P, 512, 2, 2], BF16, name="g1", align_bytes=64)
-            nc.vector.tensor_tensor(
-                out=g1[:],
-                in0=cv[:].rearrange("p v (b s) -> p b v s", s=2),
-                in1=mb[:].rearrange("p v (b s) -> p b v s", s=2),
-                op=ALU.mult,
-            )
-            st[("g", u, 1)] = g1
-
-        def quant(u, ps):
-            if ps == 0:
+        def quant(u, ps, c=FULL):
+            if ("codes", u) not in st:
                 codes = cod.tile([P, 2, 512], U32, name="codes", align_bytes=64)
                 scl = cod.tile([P, 2, 512], U8, name="scl", align_bytes=64)
                 st[("codes", u)] = (codes, scl)
             codes, scl = st[("codes", u)]
             nc.vector.quantize_mx(
-                out=codes[:, ps, :].bitcast(FP8X4),
-                scales=scl[:, ps, :],
-                in_=st[("g", u, ps)][:].rearrange("p b v s -> p (b v s)"),
+                out=codes[:, ps, c].bitcast(FP8X4),
+                scales=scl[:, ps, c],
+                in_=st[("g%d" % ps, u)][:, c].rearrange("p b v s -> p (b v s)"),
             )
 
-        def prep_w_move(f, ps):
-            wg = work.tile([P, 512, 4], BF16, name="wg", align_bytes=64)
-            for h in range(2):
-                pw = psx.tile([P, 4, 256], BF16, name="px")
-                for e in range(2):
-                    wk = w_sb[2 * h + e][:, f, :].rearrange("o (j k) -> o j k", k=8)
-                    for t in range(4):
-                        nc.tensor.transpose(pw[:, t, e * P:(e + 1) * P], wk[:, :, SLOT[ps][t]], ident[:])
-                nc.scalar.copy(out=wg[:, h * 256:(h + 1) * 256, :], in_=pw[:].rearrange("p t o -> p o t"))
-            st[("wg", f, ps)] = wg
+        def prep_w_move(f, ps, h):
+            if h == 0:
+                st[("wg", f, ps)] = work.tile([P, 512, 4], BF16, name="wg", align_bytes=64)
+            wg = st[("wg", f, ps)]
+            pw = psx.tile([P, 4, 256], BF16, name="px")
+            for e in range(2):
+                wk = w_sb[2 * h + e][:, f, :].rearrange("o (j k) -> o j k", k=8)
+                for t in range(4):
+                    nc.tensor.transpose(pw[:, t, e * P:(e + 1) * P], wk[:, :, SLOT[ps][t]], ident[:])
+            nc.scalar.copy(out=wg[:, h * 256:(h + 1) * 256, :], in_=pw[:].rearrange("p t o -> p o t"))
 
         def prep_w_quant(f, ps):
             nc.vector.quantize_mx(
@@ -227,8 +219,9 @@ def tile_kan_layer_kernel(tc, x, spline_coeffs, out):
             acc = psa.tile([P, 512], F32, name="acc")
             codes, scl = st[("codes", u)]
             n = 0
-            for ps in range(2):
-                for f in range(4):
+            for f2 in range(2):
+              for ps in range(2):
+                for f in (2 * f2, 2 * f2 + 1):
                     nc.tensor.matmul_mx(
                         out=acc[:],
                         lhsT=codes[:, ps, f * P:(f + 1) * P].bitcast(FP8X4),
@@ -246,48 +239,89 @@ def tile_kan_layer_kernel(tc, x, spline_coeffs, out):
         def ok(u):
             return 0 <= u < NU
 
+        xperm(0)
+        xperm(1)
+        for c in HALVES:
+            sig(0, c)
+            uten(0, c)
+        for c in HALVES:
+            folds(0, c)
+            wave(0, c)
+            square(0, c)
+        for h in range(2):
+            cube(0, HALVES[h])
+            turn(0, h)
+        sig(1)
+        uten(1)
+        xpair(0)
+        xperm(2)
+
         done = 0
-        for i in range(-2, NU + 4):
+        moved = 0
+        for i in range(1, NU + 2):
             a = i - 2
             b = i - 3
-            if ok(a):
+            if i == 1:
+                for h in range(2):
+                    small(0, h)
+                    combine(0, h)
+                masks(0)
+            elif i > 2 and ok(a):
                 small(a, 0)
                 small(a, 1)
                 combine(a, 0)
-            if ok(i - 1):
+            if i >= 2 and ok(i - 1):
                 wave(i - 1)
                 square(i - 1)
-            if ok(a):
+            if i > 2 and ok(a):
                 masks(a)
+                if a == NU - 1:
+                    for ps in range(2):
+                        gate(a, ps, HALVES[0])
                 combine(a, 1)
             if ok(b):
                 quant(b, 0)
-            if ok(i - 1):
+            if i >= 2 and ok(i - 1):
                 cube(i - 1)
                 turn(i - 1, 0)
                 turn(i - 1, 1)
             if ok(i):
                 folds(i)
-            if ok(a):
-                gate_first(a)
+            if ok(a) and a < NU - 1:
+                gate(a, 0)
             if ok(b):
                 quant(b, 1)
-            if ok(a):
-                gate_second(a)
+            if ok(a) and a < NU - 1:
+                gate(a, 1)
+            if a == NU - 1:
+                for ps in range(2):
+                    quant(a, ps, HALVES[0])
+                for ps in range(2):
+                    gate(a, ps, HALVES[1])
+                for ps in range(2):
+                    quant(a, ps, HALVES[1])
+                b = a
             if ok(i + 1):
                 sig(i + 1)
-            if ok(i - 1):
+            if i >= 2 and ok(i - 1):
                 xpair(i - 1)
-            if WSTEP <= i < WSTEP + 8:
-                prep_w_move((i - WSTEP) // 2, (i - WSTEP) % 2)
+            ready = []
+            while moved < 16 and moved * WSPAN < 16 * (i - WSTEP + 1) and i >= WSTEP:
+                prep_w_move(moved // 4, (moved // 2) % 2, moved % 2)
+                if moved % 2 == 1:
+                    ready.append(moved // 2)
+                moved += 1
             if ok(i + 1):
                 uten(i + 1)
-            if WSTEP <= i < WSTEP + 8:
-                prep_w_quant((i - WSTEP) // 2, (i - WSTEP) % 2)
+            for n in ready:
+                prep_w_quant(n // 2, n % 2)
+            if i == 3:
+                load_x(2)
+                load_x(3)
             if ok(i + 2):
                 xperm(i + 2)
-            if i >= WSTEP + 7:
-                for n in range(2):
+            if moved == 16:
+                for n in range(3):
                     if done <= b and done < NU:
                         mm(done)
                         done += 1

import math
from contextlib import ExitStack

import concourse.mybir as mybir
from concourse.masks import make_identity

FLOPS = 2 * 2048 * 4096 * 512

F32 = mybir.dt.float32
BF16 = mybir.dt.bfloat16
U32 = mybir.dt.uint32
U8 = mybir.dt.uint8
FP8X4 = mybir.dt.float8_e4m3fn_x4
ALU = mybir.AluOpType
ACTF = mybir.ActivationFunctionType

P = 128
NU = 16
WSTEP = 1
WSPAN = 11
MID_A = 54.0 / 512.0
HALF_A = 197.5 / 512.0
FULL = slice(0, 512)
HALVES = (slice(0, 256), slice(256, 512))
SLOT = ((0, 7, 6, 1), (4, 3, 2, 5))


def knot_x(k):
    return 0.5 * math.log(k / (11.0 - k))


def tile_kan_layer_kernel(tc, x, spline_coeffs, out):
    nc = tc.nc
    with ExitStack() as ctx:
        ctx.enter_context(nc.allow_non_contiguous_dma(reason="64-byte runs regroup the coefficients by feature class"))
        const = ctx.enter_context(tc.tile_pool(name="const", bufs=1))
        work = ctx.enter_context(tc.tile_pool(name="work", bufs=2))
        cod = ctx.enter_context(tc.tile_pool(name="cod", bufs=WSTEP + WSPAN))
        psa = ctx.enter_context(tc.psum_pool(name="psa", bufs=2))
        psf = ctx.enter_context(tc.psum_pool(name="psf", bufs=2))
        psx = ctx.enter_context(tc.psum_pool(name="psx", bufs=2))

        ident = const.tile([P, P], BF16, name="ident")
        make_identity(nc, ident[:])
        identf = const.tile([P, P], F32, name="identf")
        make_identity(nc, identf[:])
        pm = const.tile([P, P, 2], BF16, name="pm")
        nc.vector.tensor_copy(out=pm[:, :, 0], in_=ident[:])
        nc.vector.tensor_scalar(out=pm[:, :, 1], in0=ident[:], scalar1=-1.0, scalar2=None, op0=ALU.mult)

        xv = x.rearrange("(p t) i -> p t i", t=NU)
        ov = out.rearrange("(p t) o -> p t o", t=NU)
        w_sb = [const.tile([P, 4, 1024], BF16, name="w_sb%d" % ot) for ot in range(4)]
        wv = spline_coeffs.rearrange("(ot o) (g f s) k -> ot o f g (s k)", o=P, g=32, f=4, s=4)
        w_codes = const.tile([P, 4, 2, 512], U32, name="w_codes", align_bytes=64)
        w_scales = const.tile([P, 4, 2, 512], U8, name="w_scales", align_bytes=64)

        st = {}

        def load_x(c):
            xc = work.tile([P, 4, 512], BF16, name="xc")
            if c == 0:
                nc.sync.dma_start(out=xc[:, 0:1, :], in_=xv[:, 0:1, :])
                nc.sync.dma_start(out=xc[:, 1:4, :], in_=xv[:, 1:4, :])
            else:
                nc.sync.dma_start(out=xc[:], in_=xv[:, 4 * c:4 * c + 4, :])
            st[("xc", c)] = xc

        def load_w(f):
            for ot in range(4):
                nc.sync.dma_start(
                    out=w_sb[ot][:, f, :].rearrange("o (g e) -> o g e", e=32),
                    in_=wv[ot, :, f, :, :],
                )

        load_x(0)
        load_x(1)
        for f in range(4):
            load_w(f)

        def xperm(u):
            xp = work.tile([P, 512], BF16, name="xp", bufs=3)
            nc.vector.tensor_copy(
                out=xp[:].rearrange("p (f g s) -> p f g s", f=4, g=32, s=4),
                in_=st[("xc", u // 4)][:, u % 4, :].rearrange("p (g f s) -> p f g s", g=32, f=4, s=4),
            )
            st[("xp", u)] = xp

        def tile_of(key, u, shape, dtype, **kw):
            if (key, u) not in st:
                st[(key, u)] = work.tile(shape, dtype, name=key, **kw)
            return st[(key, u)]

        def sig(u, c=FULL):
            xp = st[("xp", u)]
            sg = tile_of("sg", u, [P, 2, 512], F32, bufs=3)
            nc.scalar.activation(out=sg[:, 0, c], in_=xp[:, c], func=ACTF.Sigmoid, scale=2.0)
            nc.scalar.activation(out=sg[:, 1, c], in_=xp[:, c], func=ACTF.Sigmoid, scale=-2.0)

        def xpair(u):
            xp = st[("xp", u)]
            px = psx.tile([P, 4, 256], BF16, name="px")
            for f in range(4):
                nc.tensor.matmul(px[:, f, :], lhsT=xp[:, f * P:(f + 1) * P], rhs=pm[:].rearrange("p b s -> p (b s)"), start=True, stop=True)
            x2 = work.tile([P, 1024], BF16, name="x2")
            nc.scalar.copy(out=x2[:], in_=px[:].rearrange("p f n -> p (f n)"))
            xd = work.tile([P, 1024], BF16, name="xd")
            nc.scalar.activation(out=xd[:], in_=px[:].rearrange("p f n -> p (f n)"), func=ACTF.Abs, bias=-MID_A)
            st[("x2", u)] = x2
            st[("xd", u)] = xd

        def uten(u, c=FULL):
            sg = st[("sg", u)]
            nc.vector.tensor_scalar(out=sg[:, :, c], in0=sg[:, :, c], scalar1=11.0, scalar2=10.0, op0=ALU.mult, op1=ALU.min)

        def folds(u, c=FULL):
            fh = tile_of("fh", u, [P, 2, 512], F32)
            nc.scalar.activation(out=fh[:, :, c], in_=st[("sg", u)][:, :, c], func=ACTF.Abs, bias=-7.0)
            nc.scalar.activation(out=fh[:, :, c], in_=fh[:, :, c], func=ACTF.Abs, bias=-2.0)
            nc.scalar.activation(out=fh[:, :, c], in_=fh[:, :, c], func=ACTF.Abs, bias=-2.0)

        def wave(u, c=FULL):
            z = tile_of("z", u, [P, 2, 512], F32)
            nc.vector.scalar_tensor_tensor(out=z[:, :, c], in0=st[("fh", u)][:, :, c], scalar=-1.0, in1=st[("sg", u)][:, :, c], op0=ALU.add, op1=ALU.min)

        def square(u, c=FULL):
            q = tile_of("q", u, [P, 2, 512], F32)
            nc.scalar.activation(out=q[:, :, c], in_=st[("z", u)][:, :, c], func=ACTF.Square, scale=1.0 / math.sqrt(3.0))

        def cube(u, c=FULL):
            q = st[("q", u)]
            nc.vector.scalar_tensor_tensor(out=q[:, :, c], in0=st[("z", u)][:, :, c], scalar=-1.0, in1=q[:, :, c], op0=ALU.mult, op1=ALU.mult)

        def masks(u):
            x2 = st[("x2", u)]
            m1 = work.tile([P, 2, 1024], BF16, name="m1")
            m2 = work.tile([P, 1024], BF16, name="m2")
            mb = work.tile([P, 2, 1024], BF16, name="mb")
            nc.vector.tensor_scalar(out=m1[:, 0, :], in0=x2[:], scalar1=knot_x(4), scalar2=None, op0=ALU.is_lt)
            nc.vector.tensor_scalar(out=m1[:, 1, :], in0=x2[:], scalar1=knot_x(6), scalar2=None, op0=ALU.is_gt)
            nc.vector.tensor_scalar(out=m2[:], in0=x2[:], scalar1=knot_x(2), scalar2=None, op0=ALU.is_gt)
            nc.vector.tensor_scalar(out=mb[:, 0, :], in0=st[("xd", u)][:], scalar1=HALF_A, scalar2=None, op0=ALU.is_lt)
            nc.vector.tensor_tensor(out=mb[:, 1, :], in0=m2[:], in1=m1[:, 1, :], op=ALU.subtract)
            st[("m", u)] = (m1, mb)

        def turn(u, h):
            z = st[("z", u)]
            y = st[("q", u)]
            yt = psf.tile([P, 2, 256], F32, name="yt")
            wt = psf.tile([P, 2, 256], F32, name="wt")
            for s in range(2):
                for e in range(2):
                    cols = slice((2 * h + e) * P, (2 * h + e + 1) * P)
                    dst = slice(e * P, (e + 1) * P)
                    nc.tensor.matmul(yt[:, s, dst], lhsT=y[:, s, cols], rhs=identf[:], is_transpose=True, start=True, stop=True)
                    nc.tensor.matmul(wt[:, s, dst], lhsT=z[:, 1 - s, cols], rhs=identf[:], is_transpose=True, start=True, stop=False)
                    nc.tensor.matmul(wt[:, s, dst], lhsT=y[:, 1 - s, cols], rhs=identf[:], is_transpose=True, start=False, stop=True)
            st[("t", u, h)] = (yt, wt)

        def small(u, h):
            yt, wt = st[("t", u, h)]
            sm = work.tile([P, 256, 2], F32, name="sm")
            nc.scalar.activation(out=sm[:], in_=yt[:].rearrange("p s b -> p b s"), func=ACTF.Abs, scale=0.5)
            st[("sm", u, h)] = sm

        def combine(u, h):
            if h == 0:
                st[("cv", u)] = work.tile([P, 2, 1024], BF16, name="cv")
            cv = st[("cv", u)]
            yt, wt = st[("t", u, h)]
            sm = st[("sm", u, h)]
            cols = slice(512 * h, 512 * h + 512)
            wv2 = wt[:].rearrange("p s b -> p b s")
            nc.vector.scalar_tensor_tensor(out=cv[:, 0, cols].rearrange("p (b s) -> p b s", s=2), in0=wv2, scalar=0.0, in1=sm[:], op0=ALU.max, op1=ALU.add)
            nc.vector.scalar_tensor_tensor(out=cv[:, 1, cols].rearrange("p (b s) -> p b s", s=2), in0=wv2, scalar=0.0, in1=sm[:], op0=ALU.min, op1=ALU.subtract, reverse1=True)

        def gate(u, ps, c=FULL):
            cv = st[("cv", u)]
            g = tile_of("g%d" % ps, u, [P, 512, 2, 2], BF16, align_bytes=64)
            pairs = slice(2 * c.start, 2 * c.stop)
            nc.vector.tensor_tensor(
                out=g[:, c],
                in0=cv[:, :, pairs].rearrange("p v (b s) -> p b v s", s=2),
                in1=st[("m", u)][ps][:, :, pairs].rearrange("p v (b s) -> p b v s", s=2),
                op=ALU.mult,
            )

        def quant(u, ps, c=FULL):
            if ("codes", u) not in st:
                codes = cod.tile([P, 2, 512], U32, name="codes", align_bytes=64)
                scl = cod.tile([P, 2, 512], U8, name="scl", align_bytes=64)
                st[("codes", u)] = (codes, scl)
            codes, scl = st[("codes", u)]
            nc.vector.quantize_mx(
                out=codes[:, ps, c].bitcast(FP8X4),
                scales=scl[:, ps, c],
                in_=st[("g%d" % ps, u)][:, c].rearrange("p b v s -> p (b v s)"),
            )

        def prep_w_move(f, ps, h):
            if h == 0:
                st[("wg", f, ps)] = work.tile([P, 512, 4], BF16, name="wg", align_bytes=64)
            wg = st[("wg", f, ps)]
            pw = psx.tile([P, 4, 256], BF16, name="px")
            for e in range(2):
                wk = w_sb[2 * h + e][:, f, :].rearrange("o (j k) -> o j k", k=8)
                for t in range(4):
                    nc.tensor.transpose(pw[:, t, e * P:(e + 1) * P], wk[:, :, SLOT[ps][t]], ident[:])
            nc.scalar.copy(out=wg[:, h * 256:(h + 1) * 256, :], in_=pw[:].rearrange("p t o -> p o t"))

        def prep_w_quant(f, ps):
            nc.vector.quantize_mx(
                out=w_codes[:, f, ps, :].bitcast(FP8X4),
                scales=w_scales[:, f, ps, :],
                in_=st[("wg", f, ps)][:].rearrange("p o t -> p (o t)"),
            )

        def mm(u):
            acc = psa.tile([P, 512], F32, name="acc")
            codes, scl = st[("codes", u)]
            n = 0
            for f2 in range(2):
              for ps in range(2):
                for f in (2 * f2, 2 * f2 + 1):
                    nc.tensor.matmul_mx(
                        out=acc[:],
                        lhsT=codes[:, ps, f * P:(f + 1) * P].bitcast(FP8X4),
                        lhsT_scale=scl[:, ps, f * P:(f + 1) * P],
                        rhs=w_codes[:, f, ps, :].bitcast(FP8X4),
                        rhs_scale=w_scales[:, f, ps, :],
                        start=(n == 0),
                        stop=(n == 7),
                    )
                    n += 1
            osb = work.tile([P, 512], F32, name="osb")
            nc.scalar.copy(out=osb[:], in_=acc[:])
            nc.sync.dma_start(out=ov[:, u, :], in_=osb[:])

        def ok(u):
            return 0 <= u < NU

        xperm(0)
        xperm(1)
        for c in HALVES:
            sig(0, c)
            uten(0, c)
        for c in HALVES:
            folds(0, c)
            wave(0, c)
            square(0, c)
        for h in range(2):
            cube(0, HALVES[h])
            turn(0, h)
        sig(1)
        uten(1)
        xpair(0)
        xperm(2)

        done = 0
        moved = 0
        for i in range(1, NU + 2):
            a = i - 2
            b = i - 3
            if i == 1:
                for h in range(2):
                    small(0, h)
                    combine(0, h)
                masks(0)
            elif i > 2 and ok(a):
                small(a, 0)
                small(a, 1)
                combine(a, 0)
            if i >= 2 and ok(i - 1):
                wave(i - 1)
                square(i - 1)
            if i > 2 and ok(a):
                masks(a)
                if a == NU - 1:
                    for ps in range(2):
                        gate(a, ps, HALVES[0])
                combine(a, 1)
            if ok(b):
                quant(b, 0)
            if i >= 2 and ok(i - 1):
                cube(i - 1)
                turn(i - 1, 0)
                turn(i - 1, 1)
            if ok(i):
                folds(i)
            if ok(a) and a < NU - 1:
                gate(a, 0)
            if ok(b):
                quant(b, 1)
            if ok(a) and a < NU - 1:
                gate(a, 1)
            if a == NU - 1:
                for ps in range(2):
                    quant(a, ps, HALVES[0])
                for ps in range(2):
                    gate(a, ps, HALVES[1])
                for ps in range(2):
                    quant(a, ps, HALVES[1])
                b = a
            if ok(i + 1):
                sig(i + 1)
            if i >= 2 and ok(i - 1):
                xpair(i - 1)
            ready = []
            while moved < 16 and moved * WSPAN < 16 * (i - WSTEP + 1) and i >= WSTEP:
                prep_w_move(moved // 4, (moved // 2) % 2, moved % 2)
                if moved % 2 == 1:
                    ready.append(moved // 2)
                moved += 1
            if ok(i + 1):
                uten(i + 1)
            for n in ready:
                prep_w_quant(n // 2, n % 2)
            if i == 3:
                load_x(2)
                load_x(3)
            if ok(i + 2):
                xperm(i + 2)
            if moved == 16:
                for n in range(3):
                    if done <= b and done < NU:
                        mm(done)
                        done += 1
